import numpy as np
import ml_dtypes


def mxq(x, axis, fmt="e4m3"):
    dtype, down = {"e4m3": (ml_dtypes.float8_e4m3fn, 7), "e5m2": (ml_dtypes.float8_e5m2, 14)}[fmt]
    v = np.moveaxis(np.asarray(x, np.float32).astype(ml_dtypes.bfloat16).astype(np.float64), axis, -1)
    blocks = v.reshape(v.shape[:-1] + (-1, 32))
    amax = np.abs(blocks).max(-1, keepdims=True)
    byte = np.maximum(np.where(amax > 0, np.frexp(amax)[1] - 1 + 127, 0) - down, 1)
    scale = np.exp2(byte - 127.0)
    codes = (blocks / scale).astype(np.float32).astype(dtype).astype(np.float64)
    return np.moveaxis((codes * scale).reshape(v.shape), -1, axis)


WIDE = False


def mx_kscale(k):
    if not WIDE:
        return np.ones(k)
    levels = np.array([10, -10, 5, -5, 0])
    a = np.random.permutation(np.resize(levels, k // 512 * 4)).reshape(k // 512, 4)
    idx = np.arange(k)
    return np.exp2(a[idx // 512, idx % 128 // 32])


BF16 = ml_dtypes.bfloat16


def bf(x):
    return np.asarray(x, np.float32).astype(BF16)


def f64(x):
    return np.asarray(x).astype(np.float64)


M, K, N = 1024, 2048, 2048


def ternary_quantize(w):
    thresh = 0.5 * np.abs(w).mean()
    return (w > thresh).astype(np.float64) - (w < -thresh).astype(np.float64)


def setup_inputs():
    s = mx_kscale(K)
    x = bf(np.random.standard_normal((M, K)) * s)
    weight = bf(np.random.uniform(-1.0, 1.0, (N, K)) * 1.1 / np.sqrt(K) / s)
    aw = np.abs(f64(weight))
    act = (aw > 0.5 * aw.mean()).mean(axis=0)
    c = 2.0 ** np.round(0.5 * np.log2((act * s * s).sum() / (0.75 * K)))
    return {"x": x,
            "weight": weight,
            "bias": bf(np.random.standard_normal(N) * 0.5 * np.sqrt(K) * c),
            "gamma": bf((1.0 + 0.1 * np.random.standard_normal(1)) / np.sqrt(K) / c)}


def reference(x, weight, bias, gamma):
    x = f64(x)
    weight = f64(weight)
    w_q = ternary_quantize(weight)
    w_ste = weight + (w_q - weight)
    out = (mxq(x, 1, "e4m3") @ mxq(w_ste, 1, "e4m3").T) + f64(bias)
    return out * f64(gamma)

@@ -1,0 +1,232 @@
+from contextlib import ExitStack
+
+import concourse.bass as bass
+import concourse.mybir as mybir
+import concourse.tile as tile
+from concourse.masks import make_identity
+
+F32 = mybir.dt.float32
+BF16 = mybir.dt.bfloat16
+I32 = mybir.dt.int32
+U32 = mybir.dt.uint32
+U8 = mybir.dt.uint8
+FP8X4 = mybir.dt.float8_e4m3fn_x4
+ALU = mybir.AluOpType
+ACT = mybir.ActivationFunctionType
+
+P = 128
+M, K, N = 1024, 2048, 2048
+FLOPS = 2 * M * K * N
+G = K // 512
+MT = M // P
+NB = N // P
+NC = N // 512
+ABS_MASK = 0x7FFF7FFF
+SIGN_MASK = -0x7FFF8000
+
+
+def tile_ternarylineartorch_kernel(tc, x, weight, bias, gamma, out):
+    nc = tc.nc
+    with ExitStack() as ctx:
+        ctx.enter_context(tc.manual_schedule())
+        const = ctx.enter_context(tc.tile_pool(name="const", bufs=1))
+        keep = ctx.enter_context(tc.tile_pool(name="keep", bufs=1))
+        stage = ctx.enter_context(tc.tile_pool(name="stage", bufs=4))
+        xgp = ctx.enter_context(tc.tile_pool(name="xgp", bufs=3))
+        outp = ctx.enter_context(tc.tile_pool(name="outp", bufs=5))
+        psum = ctx.enter_context(tc.psum_pool(name="psum", bufs=1))
+
+        def bank(k, name):
+            return psum.tile([P, 512], F32, tag="b%d" % k, name=name)
+
+        ident = const.tile([P, P], F32, name="ident")
+        make_identity(nc, ident[:])
+        ones_bf = const.tile([P, 32], BF16, name="ones_bf")
+        nc.vector.memset(ones_bf[:], 1.0)
+        ones_f = const.tile([P, P], F32, name="ones_f")
+        nc.vector.memset(ones_f[:], 1.0)
+        gam_bf = const.tile([P, 1], BF16, name="gam_bf")
+        nc.scalar.dma_start(out=gam_bf[:], in_=gamma.partition_broadcast(P))
+        gam_f = const.tile([P, 1], F32, name="gam_f")
+        ssum_sb = const.tile([P, 32], F32, name="ssum_sb")
+        t_sb = const.tile([P, 1], F32, name="t_sb")
+        bias_bc = const.tile([P, N], BF16, name="bias_bc")
+
+        w_t = keep.tile([P, NC, G, 1024], I32, name="w_t", align_bytes=64)
+        a_t = keep.tile([P, NC, G, 1024], I32, name="a_t", align_bytes=64)
+        w_codes = keep.tile([P, NC, G, 512], U32, name="w_codes", align_bytes=64)
+        w_sc = keep.tile([P, NC, G, 512], U8, name="w_sc", align_bytes=64)
+        x_codes = keep.tile([P, G, M], U32, name="x_codes", align_bytes=64)
+        x_sc = keep.tile([P, G, M], U8, name="x_sc", align_bytes=64)
+
+        ssum_ps = bank(0, "ssum_ps")
+        th_ps = bank(1, "th_ps")
+
+        def load(rows, name):
+            nat = stage.tile([P, K], BF16, name=name, tag="nat")
+            nc.sync.dma_start(out=nat[:], in_=rows)
+            return nat
+
+        def transposes(nat, pair, name):
+            words = nat[:].bitcast(F32)
+            banks = []
+            for h in range(2):
+                tp = bank(2 + 2 * pair + h, "%s_%d" % (name, h))
+                for j in range(4):
+                    col = 512 * h + 128 * j
+                    nc.tensor.transpose(tp[:, 128 * j : 128 * j + 128], words[:, col : col + 128], ident[:])
+                banks.append(tp)
+            return banks
+
+        def copy_out(engine_is_vector, tp, dst):
+            src = tp[:].rearrange("p (g u r) -> p g r u", g=2, u=2)
+            if engine_is_vector:
+                nc.vector.tensor_copy(out=dst, in_=src)
+            else:
+                nc.scalar.copy(out=dst, in_=src)
+
+        def w_block(s):
+            c, bb = divmod(s, 4)
+            nat = load(weight[P * s : P * s + P, :], "wn")
+            banks = transposes(nat, s % 3, "wtp")
+            for h in range(2):
+                dst = w_t[:, c, 2 * h : 2 * h + 2, 256 * bb : 256 * bb + 256].bitcast(F32)
+                dst = dst.rearrange("p g (r u) -> p g r u", u=2)
+                copy_out(h == 1 and s % 2 == 1, banks[h], dst)
+
+        def w_abs(s):
+            c, bb = divmod(s, 4)
+            nc.vector.tensor_scalar(
+                out=a_t[:, c, :, 256 * bb : 256 * bb + 256],
+                in0=w_t[:, c, :, 256 * bb : 256 * bb + 256],
+                scalar1=ABS_MASK,
+                scalar2=None,
+                op0=ALU.bitwise_and,
+            )
+
+        def w_sums(s):
+            c, bb = divmod(s, 4)
+            for g in range(G):
+                cols = a_t[:, c, g, 256 * bb : 256 * bb + 256].bitcast(BF16)
+                for j in range(4):
+                    nc.tensor.matmul(
+                        out=ssum_ps[:, 0:32],
+                        lhsT=cols[:, 128 * j : 128 * j + 128],
+                        rhs=ones_bf[:],
+                        start=(s == 0 and g == 0 and j == 0),
+                        stop=(s == NB - 1 and g == G - 1 and j == 3),
+                    )
+
+        xgs = {}
+
+        def x_tile(i):
+            nat = load(x[P * i : P * i + P, :], "xn")
+            banks = transposes(nat, 1 + i % 2, "xtp")
+            xg = xgp.tile([P, 1024], F32, name="xg", align_bytes=64)
+            for h in range(2):
+                dst = xg[:, 512 * h : 512 * h + 512].rearrange("p (g r u) -> p g r u", g=2, u=2)
+                copy_out(False, banks[h], dst)
+            xgs[i] = xg
+
+        def x_quant(i):
+            xg = xgs[i]
+            for g in range(G):
+                nc.vector.quantize_mx(
+                    out=x_codes[:, g, P * i : P * i + P].bitcast(FP8X4),
+                    scales=x_sc[:, g, P * i : P * i + P],
+                    in_=xg[:, 256 * g : 256 * g + 256].bitcast(BF16),
+                )
+
+        for s in range(NB):
+            w_block(s)
+            if s == 0:
+                nc.vector.tensor_copy(out=gam_f[:], in_=gam_bf[:])
+            if s >= 1:
+                w_abs(s - 1)
+            if s >= 2:
+                w_sums(s - 2)
+        w_abs(NB - 1)
+        w_sums(NB - 2)
+        x_tile(0)
+        w_sums(NB - 1)
+        nc.vector.tensor_copy(out=ssum_sb[:], in_=ssum_ps[:, 0:32])
+        nc.tensor.matmul(out=th_ps[:, 0:32], lhsT=ones_f[:], rhs=ssum_sb[:], start=True, stop=True)
+        nc.vector.tensor_scalar(
+            out=t_sb[:], in0=th_ps[:, 0:1], scalar1=0.5 / (N * K), scalar2=None, op0=ALU.mult
+        )
+        for i in range(1, MT):
+            x_tile(i)
+        nc.sync.dma_start(out=bias_bc[:], in_=bias.partition_broadcast(P))
+
+        def mask(q):
+            c, g = divmod(q, G)
+            a_bf = a_t[:, c, g, :].bitcast(BF16)
+            nc.vector.tensor_scalar(out=a_bf, in0=a_bf, scalar1=t_sb[:, 0:1], scalar2=None, op0=ALU.is_gt)
+
+        def signed(q):
+            c, g = divmod(q, G)
+            nc.vector.scalar_tensor_tensor(
+                out=a_t[:, c, g, :],
+                in0=w_t[:, c, g, :],
+                scalar=SIGN_MASK,
+                in1=a_t[:, c, g, :],
+                op0=ALU.bitwise_and,
+                op1=ALU.bitwise_or,
+            )
+
+        def w_quant(q):
+            c, g = divmod(q, G)
+            nc.vector.quantize_mx(
+                out=w_codes[:, c, g, :].bitcast(FP8X4),
+                scales=w_sc[:, c, g, :],
+                in_=a_t[:, c, g, :].bitcast(BF16),
+            )
+
+        accs = {}
+
+        def passes(c, h, g):
+            for j in range(4):
+                i = 4 * h + j
+                if g == 0:
+                    accs[(c, i)] = bank(4 * h + j, "acc")
+                nc.tensor.matmul_mx(
+                    out=accs[(c, i)][:],
+                    lhsT=x_codes[:, g, P * i : P * i + P].bitcast(FP8X4),
+                    lhsT_scale=x_sc[:, g, P * i : P * i + P],
+                    rhs=w_codes[:, c, g, :].bitcast(FP8X4),
+                    rhs_scale=w_sc[:, c, g, :],
+                    start=(g == 0),
+                    stop=(g == G - 1),
+                )
+
+        def epilogue(c, h):
+            for j in range(4):
+                i = 4 * h + j
+                o = outp.tile([P, 512], F32, name="o")
+                nc.vector.tensor_tensor(
+                    out=o[:], in0=accs[(c, i)][:], in1=bias_bc[:, 512 * c : 512 * c + 512], op=ALU.add
+                )
+                nc.scalar.activation(out=o[:], in_=o[:], func=ACT.Copy, scale=gam_f[:, 0:1])
+                nc.sync.dma_start(out=out[P * i : P * i + P, 512 * c : 512 * c + 512], in_=o[:])
+
+        mask(0)
+        for q in range(NC * G):
+            c, g = divmod(q, G)
+            signed(q)
+            if q + 1 < NC * G:
+                mask(q + 1)
+            if q == 0:
+                x_quant(0)
+                x_quant(1)
+            w_quant(q)
+            if q < 3:
+                x_quant(2 * q + 2)
+                x_quant(2 * q + 3)
+            if c >= 1 and g < 2:
+                epilogue(c - 1, g)
+            passes(c, 0, g)
+            if g == G - 1:
+                for gg in range(G):
+                    passes(c, 1, gg)
+        epilogue(NC - 1, 0)
+        epilogue(NC - 1, 1)

@@ -1,8 +1,6 @@
 from contextlib import ExitStack
 
-import concourse.bass as bass
 import concourse.mybir as mybir
-import concourse.tile as tile
 from concourse.masks import make_identity
 
 F32 = mybir.dt.float32
@@ -19,8 +17,8 @@ M, K, N = 1024, 2048, 2048
 FLOPS = 2 * M * K * N
 G = K // 512
 MT = M // P
-NB = N // P
 NC = N // 512
+NQ = NC * G
 ABS_MASK = 0x7FFF7FFF
 SIGN_MASK = -0x7FFF8000
 
@@ -31,9 +29,8 @@ def tile_ternarylineartorch_kernel(tc, x, weight, bias, gamma, out):
         ctx.enter_context(tc.manual_schedule())
         const = ctx.enter_context(tc.tile_pool(name="const", bufs=1))
         keep = ctx.enter_context(tc.tile_pool(name="keep", bufs=1))
-        stage = ctx.enter_context(tc.tile_pool(name="stage", bufs=4))
-        xgp = ctx.enter_context(tc.tile_pool(name="xgp", bufs=3))
-        outp = ctx.enter_context(tc.tile_pool(name="outp", bufs=5))
+        stage = ctx.enter_context(tc.tile_pool(name="stage", bufs=3))
+        xgp = ctx.enter_context(tc.tile_pool(name="xgp", bufs=2))
         psum = ctx.enter_context(tc.psum_pool(name="psum", bufs=1))
 
         def bank(k, name):
@@ -52,103 +49,112 @@ def tile_ternarylineartorch_kernel(tc, x, weight, bias, gamma, out):
         t_sb = const.tile([P, 1], F32, name="t_sb")
         bias_bc = const.tile([P, N], BF16, name="bias_bc")
 
-        w_t = keep.tile([P, NC, G, 1024], I32, name="w_t", align_bytes=64)
-        a_t = keep.tile([P, NC, G, 1024], I32, name="a_t", align_bytes=64)
-        w_codes = keep.tile([P, NC, G, 512], U32, name="w_codes", align_bytes=64)
-        w_sc = keep.tile([P, NC, G, 512], U8, name="w_sc", align_bytes=64)
-        x_codes = keep.tile([P, G, M], U32, name="x_codes", align_bytes=64)
-        x_sc = keep.tile([P, G, M], U8, name="x_sc", align_bytes=64)
+        w_t = [keep.tile([P, 1024], I32, name="w_t%d" % q, align_bytes=64) for q in range(NQ)]
+        a_t = [keep.tile([P, 1024], I32, name="a_t%d" % q, align_bytes=64) for q in range(NQ)]
+        w_codes = [keep.tile([P, 512], U32, name="w_codes%d" % q, align_bytes=64) for q in range(NQ)]
+        w_sc = [keep.tile([P, 512], U8, name="w_sc%d" % q, align_bytes=64) for q in range(NQ)]
+        x_codes = [keep.tile([P, G, 512], U32, name="x_codes%d" % h, align_bytes=64) for h in range(2)]
+        x_sc = [keep.tile([P, G, 512], U8, name="x_sc%d" % h, align_bytes=64) for h in range(2)]
 
         ssum_ps = bank(0, "ssum_ps")
         th_ps = bank(1, "th_ps")
 
-        def load(rows, name):
-            nat = stage.tile([P, K], BF16, name=name, tag="nat")
-            nc.sync.dma_start(out=nat[:], in_=rows)
-            return nat
+        def four_transposes(tp, sources):
+            for j in range(4):
+                nc.tensor.transpose(tp[:, 128 * j : 128 * j + 128], sources[j], ident[:])
 
-        def transposes(nat, pair, name):
-            words = nat[:].bitcast(F32)
-            banks = []
-            for h in range(2):
-                tp = bank(2 + 2 * pair + h, "%s_%d" % (name, h))
-                for j in range(4):
-                    col = 512 * h + 128 * j
-                    nc.tensor.transpose(tp[:, 128 * j : 128 * j + 128], words[:, col : col + 128], ident[:])
-                banks.append(tp)
-            return banks
-
-        def copy_out(engine_is_vector, tp, dst):
-            src = tp[:].rearrange("p (g u r) -> p g r u", g=2, u=2)
-            if engine_is_vector:
+        def copy_out(on_vector, tp, dst):
+            src = tp[:].rearrange("p (b u r) -> p b r u", b=2, u=2)
+            dst = dst.rearrange("p (b r u) -> p b r u", b=2, u=2)
+            if on_vector:
                 nc.vector.tensor_copy(out=dst, in_=src)
             else:
                 nc.scalar.copy(out=dst, in_=src)
 
-        def w_block(s):
-            c, bb = divmod(s, 4)
-            nat = load(weight[P * s : P * s + P, :], "wn")
-            banks = transposes(nat, s % 3, "wtp")
-            for h in range(2):
-                dst = w_t[:, c, 2 * h : 2 * h + 2, 256 * bb : 256 * bb + 256].bitcast(F32)
-                dst = dst.rearrange("p g (r u) -> p g r u", u=2)
-                copy_out(h == 1 and s % 2 == 1, banks[h], dst)
+        nats = {}
 
-        def w_abs(s):
-            c, bb = divmod(s, 4)
+        def w_load(d):
+            c, gp = divmod(d, 2)
+            nat = stage.tile([P, 4, 1024], BF16, name="wn", tag="nat")
+            rows = weight[512 * c : 512 * c + 512, 1024 * gp : 1024 * gp + 1024]
+            nc.sync.dma_start(out=nat[:], in_=rows.rearrange("(b p) k -> p b k", p=P))
+            nats[d] = nat
+
+        def w_unit(q):
+            nat = nats[q // 2]
+            gg = q % 2
+            for h in range(2):
+                tp = bank(2 + 2 * (q % 3) + h, "wtp%d" % h)
+                srcs = []
+                for bl in range(2):
+                    words = nat[:, 2 * h + bl, :].bitcast(F32)
+                    for u in range(2):
+                        col = 256 * gg + 128 * u
+                        srcs.append(words[:, col : col + 128])
+                four_transposes(tp, srcs)
+                copy_out(h == 1 and q % 2 == 1, tp, w_t[q][:, 512 * h : 512 * h + 512].bitcast(F32))
+
+        def w_abs(q):
             nc.vector.tensor_scalar(
-                out=a_t[:, c, :, 256 * bb : 256 * bb + 256],
-                in0=w_t[:, c, :, 256 * bb : 256 * bb + 256],
-                scalar1=ABS_MASK,
-                scalar2=None,
-                op0=ALU.bitwise_and,
+                out=a_t[q][:], in0=w_t[q][:], scalar1=ABS_MASK, scalar2=None, op0=ALU.bitwise_and
             )
 
-        def w_sums(s):
-            c, bb = divmod(s, 4)
-            for g in range(G):
-                cols = a_t[:, c, g, 256 * bb : 256 * bb + 256].bitcast(BF16)
-                for j in range(4):
-                    nc.tensor.matmul(
-                        out=ssum_ps[:, 0:32],
-                        lhsT=cols[:, 128 * j : 128 * j + 128],
-                        rhs=ones_bf[:],
-                        start=(s == 0 and g == 0 and j == 0),
-                        stop=(s == NB - 1 and g == G - 1 and j == 3),
-                    )
+        def w_sums(q):
+            cols = a_t[q][:].bitcast(BF16)
+            for j in range(16):
+                nc.tensor.matmul(
+                    out=ssum_ps[:, 0:32],
+                    lhsT=cols[:, 128 * j : 128 * j + 128],
+                    rhs=ones_bf[:],
+                    start=(q == 0 and j == 0),
+                    stop=(q == NQ - 1 and j == 15),
+                )
 
+        xnats = {}
         xgs = {}
 
+        def x_load(ip):
+            nat = stage.tile([P, 2, K], BF16, name="xn", tag="nat")
+            nc.sync.dma_start(
+                out=nat[:], in_=x[256 * ip : 256 * ip + 256, :].rearrange("(t p) k -> p t k", p=P)
+            )
+            xnats[ip] = nat
+
         def x_tile(i):
-            nat = load(x[P * i : P * i + P, :], "xn")
-            banks = transposes(nat, 1 + i % 2, "xtp")
+            words = xnats[i // 2][:, i % 2, :].bitcast(F32)
             xg = xgp.tile([P, 1024], F32, name="xg", align_bytes=64)
             for h in range(2):
-                dst = xg[:, 512 * h : 512 * h + 512].rearrange("p (g r u) -> p g r u", g=2, u=2)
-                copy_out(False, banks[h], dst)
+                tp = bank(4 + 2 * (i % 2) + h, "xtp%d" % h)
+                four_transposes(tp, [words[:, 512 * h + 128 * j : 512 * h + 128 * j + 128] for j in range(4)])
+                copy_out(False, tp, xg[:, 512 * h : 512 * h + 512])
             xgs[i] = xg
 
         def x_quant(i):
-            xg = xgs[i]
+            h, j = divmod(i, 4)
             for g in range(G):
                 nc.vector.quantize_mx(
-                    out=x_codes[:, g, P * i : P * i + P].bitcast(FP8X4),
-                    scales=x_sc[:, g, P * i : P * i + P],
-                    in_=xg[:, 256 * g : 256 * g + 256].bitcast(BF16),
+                    out=x_codes[h][:, g, P * j : P * j + P].bitcast(FP8X4),
+                    scales=x_sc[h][:, g, P * j : P * j + P],
+                    in_=xgs[i][:, 256 * g : 256 * g + 256].bitcast(BF16),
                 )
 
-        for s in range(NB):
-            w_block(s)
-            if s == 0:
+        for q in range(NQ):
+            if q % 2 == 0:
+                w_load(q // 2)
+            w_unit(q)
+            if q == 0:
                 nc.vector.tensor_copy(out=gam_f[:], in_=gam_bf[:])
-            if s >= 1:
-                w_abs(s - 1)
-            if s >= 2:
-                w_sums(s - 2)
-        w_abs(NB - 1)
-        w_sums(NB - 2)
+            if q >= 1:
+                w_abs(q - 1)
+            if q >= 2:
+                w_sums(q - 2)
+        for ip in range(MT // 2):
+            x_load(ip)
+        nc.sync.dma_start(out=bias_bc[:], in_=bias.partition_broadcast(P))
+        w_abs(NQ - 1)
+        w_sums(NQ - 2)
         x_tile(0)
-        w_sums(NB - 1)
+        w_sums(NQ - 1)
         nc.vector.tensor_copy(out=ssum_sb[:], in_=ssum_ps[:, 0:32])
         nc.tensor.matmul(out=th_ps[:, 0:32], lhsT=ones_f[:], rhs=ssum_sb[:], start=True, stop=True)
         nc.vector.tensor_scalar(
@@ -156,64 +162,65 @@ def tile_ternarylineartorch_kernel(tc, x, weight, bias, gamma, out):
         )
         for i in range(1, MT):
             x_tile(i)
-        nc.sync.dma_start(out=bias_bc[:], in_=bias.partition_broadcast(P))
 
         def mask(q):
-            c, g = divmod(q, G)
-            a_bf = a_t[:, c, g, :].bitcast(BF16)
+            a_bf = a_t[q][:].bitcast(BF16)
             nc.vector.tensor_scalar(out=a_bf, in0=a_bf, scalar1=t_sb[:, 0:1], scalar2=None, op0=ALU.is_gt)
 
         def signed(q):
-            c, g = divmod(q, G)
             nc.vector.scalar_tensor_tensor(
-                out=a_t[:, c, g, :],
-                in0=w_t[:, c, g, :],
+                out=a_t[q][:],
+                in0=w_t[q][:],
                 scalar=SIGN_MASK,
-                in1=a_t[:, c, g, :],
+                in1=a_t[q][:],
                 op0=ALU.bitwise_and,
                 op1=ALU.bitwise_or,
             )
 
         def w_quant(q):
-            c, g = divmod(q, G)
             nc.vector.quantize_mx(
-                out=w_codes[:, c, g, :].bitcast(FP8X4),
-                scales=w_sc[:, c, g, :],
-                in_=a_t[:, c, g, :].bitcast(BF16),
+                out=w_codes[q][:].bitcast(FP8X4), scales=w_sc[q][:], in_=a_t[q][:].bitcast(BF16)
             )
 
         accs = {}
 
         def passes(c, h, g):
             for j in range(4):
-                i = 4 * h + j
                 if g == 0:
-                    accs[(c, i)] = bank(4 * h + j, "acc")
+                    accs[(c, h, j)] = bank(4 * h + j, "acc")
                 nc.tensor.matmul_mx(
-                    out=accs[(c, i)][:],
-                    lhsT=x_codes[:, g, P * i : P * i + P].bitcast(FP8X4),
-                    lhsT_scale=x_sc[:, g, P * i : P * i + P],
-                    rhs=w_codes[:, c, g, :].bitcast(FP8X4),
-                    rhs_scale=w_sc[:, c, g, :],
+                    out=accs[(c, h, j)][:],
+                    lhsT=x_codes[h][:, g, P * j : P * j + P].bitcast(FP8X4),
+                    lhsT_scale=x_sc[h][:, g, P * j : P * j + P],
+                    rhs=w_codes[G * c + g][:].bitcast(FP8X4),
+                    rhs_scale=w_sc[G * c + g][:],
                     start=(g == 0),
                     stop=(g == G - 1),
                 )
 
+        spare = [0]
+
+        def out_tile():
+            k = spare[0] % 8
+            spare[0] += 1
+            tag = ("w_t%d" if k % 2 == 0 else "a_t%d") % (k // 2)
+            return keep.tile([P, 512], F32, name="o", tag=tag, align_bytes=64)
+
         def epilogue(c, h):
             for j in range(4):
                 i = 4 * h + j
-                o = outp.tile([P, 512], F32, name="o")
+                o = out_tile()
                 nc.vector.tensor_tensor(
-                    out=o[:], in0=accs[(c, i)][:], in1=bias_bc[:, 512 * c : 512 * c + 512], op=ALU.add
+                    out=o[:], in0=accs[(c, h, j)][:], in1=bias_bc[:, 512 * c : 512 * c + 512], op=ALU.add
                 )
                 nc.scalar.activation(out=o[:], in_=o[:], func=ACT.Copy, scale=gam_f[:, 0:1])
                 nc.sync.dma_start(out=out[P * i : P * i + P, 512 * c : 512 * c + 512], in_=o[:])
 
         mask(0)
-        for q in range(NC * G):
+        for q in range(NQ):
             c, g = divmod(q, G)
             signed(q)
-            if q + 1 < NC * G:
+            if q + 1 < NQ:
                 mask(q + 1)
             if q == 0:
                 x_quant(0)

@@ -38,14 +38,14 @@ def tile_ternarylineartorch_kernel(tc, x, weight, bias, gamma, out):
 
         ident = const.tile([P, P], F32, name="ident")
         make_identity(nc, ident[:])
-        ones_bf = const.tile([P, 32], BF16, name="ones_bf")
+        ones_bf = const.tile([P, 64], BF16, name="ones_bf")
         nc.vector.memset(ones_bf[:], 1.0)
         ones_f = const.tile([P, P], F32, name="ones_f")
         nc.vector.memset(ones_f[:], 1.0)
         gam_bf = const.tile([P, 1], BF16, name="gam_bf")
         nc.scalar.dma_start(out=gam_bf[:], in_=gamma.partition_broadcast(P))
         gam_f = const.tile([P, 1], F32, name="gam_f")
-        ssum_sb = const.tile([P, 32], F32, name="ssum_sb")
+        ssum_sb = const.tile([P, 64], F32, name="ssum_sb")
         t_sb = const.tile([P, 1], F32, name="t_sb")
         bias_bc = const.tile([P, N], BF16, name="bias_bc")
 
@@ -103,7 +103,7 @@ def tile_ternarylineartorch_kernel(tc, x, weight, bias, gamma, out):
             cols = a_t[q][:].bitcast(BF16)
             for j in range(16):
                 nc.tensor.matmul(
-                    out=ssum_ps[:, 0:32],
+                    out=ssum_ps[:, 0:64],
                     lhsT=cols[:, 128 * j : 128 * j + 128],
                     rhs=ones_bf[:],
                     start=(q == 0 and j == 0),
@@ -155,8 +155,8 @@ def tile_ternarylineartorch_kernel(tc, x, weight, bias, gamma, out):
         w_sums(NQ - 2)
         x_tile(0)
         w_sums(NQ - 1)
-        nc.vector.tensor_copy(out=ssum_sb[:], in_=ssum_ps[:, 0:32])
-        nc.tensor.matmul(out=th_ps[:, 0:32], lhsT=ones_f[:], rhs=ssum_sb[:], start=True, stop=True)
+        nc.vector.tensor_copy(out=ssum_sb[:], in_=ssum_ps[:, 0:64])
+        nc.tensor.matmul(out=th_ps[:, 0:64], lhsT=ones_f[:], rhs=ssum_sb[:], start=True, stop=True)
         nc.vector.tensor_scalar(
             out=t_sb[:], in0=th_ps[:, 0:1], scalar1=0.5 / (N * K), scalar2=None, op0=ALU.mult
         )

@@ -21,6 +21,25 @@ NC = N // 512
 NQ = NC * G
 ABS_MASK = 0x7FFF7FFF
 SIGN_MASK = -0x7FFF8000
+NSUM = 32
+EV = {0: [("xq", 0), ("xq", 1), ("xq", 2), ("xq", 3), ("ps", 0, 0, 0), ("xt", 4), ("xt", 5), ("xt", 6), ("xt", 7)],
+      1: [("ps", 0, 0, 1)],
+      2: [("xq", 4), ("xq", 5), ("xq", 6), ("xq", 7), ("ps", 0, 0, 2), ("pv", 0, 1, 0), ("pv", 0, 1, 1), ("pv", 0, 1, 2)],
+      3: [("ps", 0, 0, 3), ("s1", 0, 0), ("pv", 0, 1, 3)],
+      4: [("ea", 0, 1), ("bt", 0, 0), ("s2", 0, 0), ("pv", 1, 1, 0), ("eg", 0, 1), ("ps", 1, 0, 0)],
+      5: [("ps", 1, 0, 1), ("pv", 1, 1, 1)],
+      6: [("ps", 1, 0, 2), ("pv", 1, 1, 2)],
+      7: [("ps", 1, 0, 3), ("s1", 1, 0), ("pv", 1, 1, 3)],
+      8: [("ea", 1, 1), ("bt", 1, 0), ("s2", 1, 0), ("pv", 2, 1, 0), ("eg", 1, 1), ("ps", 2, 0, 0)],
+      9: [("ps", 2, 0, 1), ("pv", 2, 1, 1)],
+      10: [("ps", 2, 0, 2), ("pv", 2, 1, 2)],
+      11: [("ps", 2, 0, 3), ("s1", 2, 0), ("pv", 2, 1, 3)],
+      12: [("ea", 2, 1), ("bt", 2, 0), ("s2", 2, 0), ("pv", 3, 1, 0), ("eg", 2, 1), ("pv", 3, 0, 0)],
+      13: [("pv", 3, 0, 1), ("pv", 3, 1, 1)],
+      14: [("pv", 3, 0, 2), ("pv", 3, 1, 2)],
+      15: [("pv", 3, 0, 3), ("pv", 3, 1, 3)],
+      16: [("el", 3, 0), ("el", 3, 1)]}
+PRE = []
 
 
 def tile_ternarylineartorch_kernel(tc, x, weight, bias, gamma, out):
@@ -29,8 +48,7 @@ def tile_ternarylineartorch_kernel(tc, x, weight, bias, gamma, out):
         ctx.enter_context(tc.manual_schedule())
         const = ctx.enter_context(tc.tile_pool(name="const", bufs=1))
         keep = ctx.enter_context(tc.tile_pool(name="keep", bufs=1))
-        stage = ctx.enter_context(tc.tile_pool(name="stage", bufs=3))
-        xgp = ctx.enter_context(tc.tile_pool(name="xgp", bufs=2))
+        xgp = ctx.enter_context(tc.tile_pool(name="xgp", bufs=4))
         psum = ctx.enter_context(tc.psum_pool(name="psum", bufs=1))
 
         def bank(k, name):
@@ -38,20 +56,25 @@ def tile_ternarylineartorch_kernel(tc, x, weight, bias, gamma, out):
 
         ident = const.tile([P, P], F32, name="ident")
         make_identity(nc, ident[:])
-        ones_bf = const.tile([P, 64], BF16, name="ones_bf")
+        ones_bf = const.tile([P, NSUM], BF16, name="ones_bf")
         nc.vector.memset(ones_bf[:], 1.0)
         ones_f = const.tile([P, P], F32, name="ones_f")
         nc.vector.memset(ones_f[:], 1.0)
         gam_bf = const.tile([P, 1], BF16, name="gam_bf")
         nc.scalar.dma_start(out=gam_bf[:], in_=gamma.partition_broadcast(P))
         gam_f = const.tile([P, 1], F32, name="gam_f")
-        ssum_sb = const.tile([P, 64], F32, name="ssum_sb")
+        brow_bf = const.tile([P, P], BF16, name="brow_bf")
+        nc.vector.memset(brow_bf[:], 0.0)
+        nc.scalar.dma_start(out=brow_bf[0:16, :], in_=bias.rearrange("(b p) -> b p", p=P))
+        brow_f = const.tile([P, P], F32, name="brow_f")
+        bias_col = const.tile([P, 16], F32, name="bias_col")
+        ssum_sb = const.tile([P, NSUM], F32, name="ssum_sb")
         t_sb = const.tile([P, 1], F32, name="t_sb")
         bias_bc = const.tile([P, N], BF16, name="bias_bc")
 
         w_t = [keep.tile([P, 1024], I32, name="w_t%d" % q, align_bytes=64) for q in range(NQ)]
         a_t = [keep.tile([P, 1024], I32, name="a_t%d" % q, align_bytes=64) for q in range(NQ)]
-        w_codes = [keep.tile([P, 512], U32, name="w_codes%d" % q, align_bytes=64) for q in range(NQ)]
+        w_codes = [keep.tile([P, 512], U32, name="w_codes%d" % q, align_bytes=64) for q in range(4)]
         w_sc = [keep.tile([P, 512], U8, name="w_sc%d" % q, align_bytes=64) for q in range(NQ)]
         x_codes = [keep.tile([P, G, 512], U32, name="x_codes%d" % h, align_bytes=64) for h in range(2)]
         x_sc = [keep.tile([P, G, 512], U8, name="x_sc%d" % h, align_bytes=64) for h in range(2)]
@@ -72,13 +95,8 @@ def tile_ternarylineartorch_kernel(tc, x, weight, bias, gamma, out):
                 nc.scalar.copy(out=dst, in_=src)
 
         nats = {}
-
-        def w_load(d):
-            c, gp = divmod(d, 2)
-            nat = stage.tile([P, 4, 1024], BF16, name="wn", tag="nat")
-            rows = weight[512 * c : 512 * c + 512, 1024 * gp : 1024 * gp + 1024]
-            nc.sync.dma_start(out=nat[:], in_=rows.rearrange("(b p) k -> p b k", p=P))
-            nats[d] = nat
+        xnats = {}
+        xgs = {}
 
         def w_unit(q):
             nat = nats[q // 2]
@@ -92,7 +110,7 @@ def tile_ternarylineartorch_kernel(tc, x, weight, bias, gamma, out):
                         col = 256 * gg + 128 * u
                         srcs.append(words[:, col : col + 128])
                 four_transposes(tp, srcs)
-                copy_out(h == 1 and q % 2 == 1, tp, w_t[q][:, 512 * h : 512 * h + 512].bitcast(F32))
+                copy_out(h == 1 and (q % 2 == 1 or q >= NQ - 2), tp, w_t[q][:, 512 * h : 512 * h + 512].bitcast(F32))
 
         def w_abs(q):
             nc.vector.tensor_scalar(
@@ -103,22 +121,12 @@ def tile_ternarylineartorch_kernel(tc, x, weight, bias, gamma, out):
             cols = a_t[q][:].bitcast(BF16)
             for j in range(16):
                 nc.tensor.matmul(
-                    out=ssum_ps[:, 0:64],
+                    out=ssum_ps[:, 0:NSUM],
                     lhsT=cols[:, 128 * j : 128 * j + 128],
                     rhs=ones_bf[:],
                     start=(q == 0 and j == 0),
                     stop=(q == NQ - 1 and j == 15),
                 )
-
-        xnats = {}
-        xgs = {}
-
-        def x_load(ip):
-            nat = stage.tile([P, 2, K], BF16, name="xn", tag="nat")
-            nc.sync.dma_start(
-                out=nat[:], in_=x[256 * ip : 256 * ip + 256, :].rearrange("(t p) k -> p t k", p=P)
-            )
-            xnats[ip] = nat
 
         def x_tile(i):
             words = xnats[i // 2][:, i % 2, :].bitcast(F32)
@@ -137,31 +145,6 @@ def tile_ternarylineartorch_kernel(tc, x, weight, bias, gamma, out):
                     scales=x_sc[h][:, g, P * j : P * j + P],
                     in_=xgs[i][:, 256 * g : 256 * g + 256].bitcast(BF16),
                 )
-
-        for q in range(NQ):
-            if q % 2 == 0:
-                w_load(q // 2)
-            w_unit(q)
-            if q == 0:
-                nc.vector.tensor_copy(out=gam_f[:], in_=gam_bf[:])
-            if q >= 1:
-                w_abs(q - 1)
-            if q >= 2:
-                w_sums(q - 2)
-        for ip in range(MT // 2):
-            x_load(ip)
-        nc.sync.dma_start(out=bias_bc[:], in_=bias.partition_broadcast(P))
-        w_abs(NQ - 1)
-        w_sums(NQ - 2)
-        x_tile(0)
-        w_sums(NQ - 1)
-        nc.vector.tensor_copy(out=ssum_sb[:], in_=ssum_ps[:, 0:64])
-        nc.tensor.matmul(out=th_ps[:, 0:64], lhsT=ones_f[:], rhs=ssum_sb[:], start=True, stop=True)
-        nc.vector.tensor_scalar(
-            out=t_sb[:], in0=th_ps[:, 0:1], scalar1=0.5 / (N * K), scalar2=None, op0=ALU.mult
-        )
-        for i in range(1, MT):
-            x_tile(i)
 
         def mask(q):
             a_bf = a_t[q][:].bitcast(BF16)
@@ -184,56 +167,182 @@ def tile_ternarylineartorch_kernel(tc, x, weight, bias, gamma, out):
 
         accs = {}
 
-        def passes(c, h, g):
+        def passes(c, h, g, route):
+            q = G * c + g
             for j in range(4):
                 if g == 0:
                     accs[(c, h, j)] = bank(4 * h + j, "acc")
-                nc.tensor.matmul_mx(
-                    out=accs[(c, h, j)][:],
-                    lhsT=x_codes[h][:, g, P * j : P * j + P].bitcast(FP8X4),
-                    lhsT_scale=x_sc[h][:, g, P * j : P * j + P],
-                    rhs=w_codes[G * c + g][:].bitcast(FP8X4),
-                    rhs_scale=w_sc[G * c + g][:],
-                    start=(g == 0),
-                    stop=(g == G - 1),
-                )
+                if route == "V":
+                    nc.tensor.matmul_mx(
+                        out=accs[(c, h, j)][:],
+                        lhsT=x_codes[h][:, g, P * j : P * j + P].bitcast(FP8X4),
+                        lhsT_scale=x_sc[h][:, g, P * j : P * j + P],
+                        rhs=w_codes[q][:].bitcast(FP8X4),
+                        rhs_scale=w_sc[q][:],
+                        start=(g == 0),
+                        stop=(g == G - 1),
+                    )
+                else:
+                    nc.tensor.matmul_mx(
+                        out=accs[(c, h, j)][:],
+                        lhsT=w_codes[q][:, P * j : P * j + P].bitcast(FP8X4),
+                        lhsT_scale=w_sc[q][:, P * j : P * j + P],
+                        rhs=x_codes[h][:, g, :].bitcast(FP8X4),
+                        rhs_scale=x_sc[h][:, g, :],
+                        start=(g == 0),
+                        stop=(g == G - 1),
+                    )
 
-        spare = [0]
+        def store(c, h, jp, o):
+            r0 = 512 * h + 256 * jp
+            nc.sync.dma_start(
+                out=out[r0 : r0 + 256, 512 * c : 512 * c + 512].rearrange("(t p) n -> p t n", p=P), in_=o[:]
+            )
 
-        def out_tile():
-            k = spare[0] % 8
-            spare[0] += 1
-            tag = ("w_t%d" if k % 2 == 0 else "a_t%d") % (k // 2)
-            return keep.tile([P, 512], F32, name="o", tag=tag, align_bytes=64)
+        ovs = {}
 
-        def epilogue(c, h):
+        def epilogue_add(c, h):
+            for jp in range(2):
+                o = keep.tile([P, 2, 512], F32, name="ov", tag="w_t%d" % (2 * h + jp), align_bytes=64)
+                for t in range(2):
+                    nc.vector.tensor_tensor(
+                        out=o[:, t, :],
+                        in0=accs[(c, h, 2 * jp + t)][:],
+                        in1=bias_bc[:, 512 * c : 512 * c + 512],
+                        op=ALU.add,
+                    )
+                ovs[(c, h, jp)] = o
+
+        def epilogue_gain(c, h):
+            for jp in range(2):
+                o = ovs[(c, h, jp)]
+                nc.scalar.activation(out=o[:], in_=o[:], func=ACT.Copy, scale=gam_f[:, 0:1])
+                store(c, h, jp, o)
+
+        def epilogue_last(c, h):
             for j in range(4):
                 i = 4 * h + j
-                o = out_tile()
+                o = keep.tile([P, 512], F32, name="ol", tag="%s_t%d" % ("wa"[h], 4 + j), align_bytes=64)
                 nc.vector.tensor_tensor(
                     out=o[:], in0=accs[(c, h, j)][:], in1=bias_bc[:, 512 * c : 512 * c + 512], op=ALU.add
                 )
                 nc.scalar.activation(out=o[:], in_=o[:], func=ACT.Copy, scale=gam_f[:, 0:1])
                 nc.sync.dma_start(out=out[P * i : P * i + P, 512 * c : 512 * c + 512], in_=o[:])
 
-        mask(0)
-        for q in range(NQ):
-            c, g = divmod(q, G)
+        ys = {}
+
+        def s_first(c, h):
+            for jp in range(2):
+                y = keep.tile([P, 2, 512], F32, name="y", tag="a_t%d" % (2 * h + jp), align_bytes=64)
+                for t in range(2):
+                    nb = 4 * c + 2 * jp + t
+                    nc.scalar.activation(
+                        out=y[:, t, :],
+                        in_=accs[(c, h, 2 * jp + t)][:],
+                        func=ACT.Identity,
+                        bias=bias_col[:, nb : nb + 1],
+                        scale=1.0,
+                    )
+                ys[(c, h, jp)] = y
+
+        backs = {}
+
+        def back(c, h):
+            for j in range(4):
+                bt = bank(4 * h + j, "bt")
+                four_transposes(bt, [ys[(c, h, nbl // 2)][:, nbl % 2, P * j : P * j + P] for nbl in range(4)])
+                backs[(c, h, j)] = bt
+
+        def s_second(c, h):
+            for jp in range(2):
+                o = keep.tile([P, 2, 512], F32, name="os", tag="w_t%d" % (2 * h + jp), align_bytes=64)
+                for t in range(2):
+                    nc.scalar.activation(
+                        out=o[:, t, :], in_=backs[(c, h, 2 * jp + t)][:], func=ACT.Copy, scale=gam_f[:, 0:1]
+                    )
+                store(c, h, jp, o)
+
+
+        def event(e):
+            k = e[0]
+            if k == "xq":
+                x_quant(e[1])
+            elif k == "xt":
+                x_tile(e[1])
+            elif k == "pv":
+                passes(e[1], e[2], e[3], "V")
+            elif k == "ps":
+                passes(e[1], e[2], e[3], "S")
+            elif k == "s1":
+                s_first(e[1], e[2])
+            elif k == "bt":
+                back(e[1], e[2])
+            elif k == "s2":
+                s_second(e[1], e[2])
+            elif k == "ea":
+                epilogue_add(e[1], e[2])
+            elif k == "eg":
+                epilogue_gain(e[1], e[2])
+            elif k == "el":
+                epilogue_last(e[1], e[2])
+
+        def step(q):
             signed(q)
             if q + 1 < NQ:
                 mask(q + 1)
-            if q == 0:
-                x_quant(0)
-                x_quant(1)
             w_quant(q)
-            if q < 3:
-                x_quant(2 * q + 2)
-                x_quant(2 * q + 3)
-            if c >= 1 and g < 2:
-                epilogue(c - 1, g)
-            passes(c, 0, g)
-            if g == G - 1:
-                for gg in range(G):
-                    passes(c, 1, gg)
-        epilogue(NC - 1, 0)
-        epilogue(NC - 1, 1)
+            for e in EV.get(q, []):
+                event(e)
+
+        with tc.tile_pool(name="stage", bufs=5) as stage:
+            for d in range(NQ // 2):
+                c, gp = divmod(d, 2)
+                nat = stage.tile([P, 4, 1024], BF16, name="wn", tag="nat")
+                rows = weight[512 * c : 512 * c + 512, 1024 * gp : 1024 * gp + 1024]
+                nc.sync.dma_start(out=nat[:], in_=rows.rearrange("(b p) k -> p b k", p=P))
+                nats[d] = nat
+                for q in (2 * d, 2 * d + 1):
+                    if q >= 1:
+                        w_abs(q - 1)
+                    w_unit(q)
+                    if q == 0:
+                        nc.vector.tensor_copy(out=gam_f[:], in_=gam_bf[:])
+                        nc.vector.tensor_copy(out=brow_f[:], in_=brow_bf[:])
+                    if q >= 3:
+                        w_sums(q - 3)
+                    if q == 2:
+                        nc.tensor.transpose(th_ps[:, 0:128], brow_f[:], ident[:])
+                        nc.vector.tensor_copy(out=bias_col[:], in_=th_ps[:, 0:16])
+            for ip in range(MT // 2):
+                nat = stage.tile([P, 2, K], BF16, name="xn", tag="nat")
+                nc.sync.dma_start(
+                    out=nat[:], in_=x[256 * ip : 256 * ip + 256, :].rearrange("(t p) k -> p t k", p=P)
+                )
+                xnats[ip] = nat
+            nc.sync.dma_start(out=bias_bc[:], in_=bias.partition_broadcast(P))
+            w_abs(NQ - 1)
+            for q in range(NQ - 3, NQ):
+                if q == NQ - 1:
+                    for i in range(0):
+                        x_tile(i)
+                w_sums(q)
+            nc.vector.tensor_copy(out=ssum_sb[:], in_=ssum_ps[:, 0:NSUM])
+            th2_ps = bank(1, "th2_ps")
+            nc.tensor.matmul(out=th2_ps[:, 0:NSUM], lhsT=ones_f[:], rhs=ssum_sb[:], start=True, stop=True)
+            nc.vector.tensor_scalar(
+                out=t_sb[:], in0=th2_ps[:, 0:1], scalar1=0.5 / (N * K), scalar2=None, op0=ALU.mult
+            )
+            for i in range(0, 4):
+                x_tile(i)
+            mask(0)
+            for e in PRE:
+                event(e)
+            for q in range(2):
+                step(q)
+        codes = ctx.enter_context(tc.tile_pool(name="codes", bufs=1))
+        for q in range(4, NQ):
+            w_codes.append(codes.tile([P, 512], U32, name="w_codes%d" % q, align_bytes=64))
+        for q in range(2, NQ):
+            step(q)
+        for e in EV.get(NQ, []):
+            event(e)

@@ -21,6 +21,7 @@ NC = N // 512
 NQ = NC * G
 ABS_MASK = 0x7FFF7FFF
 SIGN_MASK = -0x7FFF8000
+VSH = 7
 NSUM = 32
 EV = {0: [("xq", 0), ("xq", 1), ("xq", 2), ("xq", 3), ("ps", 0, 0, 0), ("xt", 4), ("xt", 5), ("xt", 6), ("xt", 7)],
       1: [("ps", 0, 0, 1)],
@@ -68,6 +69,10 @@ def tile_ternarylineartorch_kernel(tc, x, weight, bias, gamma, out):
         nc.scalar.dma_start(out=brow_bf[0:16, :], in_=bias.rearrange("(b p) -> b p", p=P))
         brow_f = const.tile([P, P], F32, name="brow_f")
         bias_col = const.tile([P, 16], F32, name="bias_col")
+        vs = const.tile([P, NQ], F32, name="vs")
+        nc.vector.memset(vs[:], 0.0)
+        vsum = const.tile([P, 1], F32, name="vsum")
+        junk = const.tile([P, 128 * VSH], BF16, name="junk")
         ssum_sb = const.tile([P, NSUM], F32, name="ssum_sb")
         t_sb = const.tile([P, 1], F32, name="t_sb")
         bias_bc = const.tile([P, N], BF16, name="bias_bc")
@@ -99,8 +104,7 @@ def tile_ternarylineartorch_kernel(tc, x, weight, bias, gamma, out):
         xgs = {}
 
         def w_unit(q):
-            nat = nats[q // 2]
-            gg = q % 2
+            nat, gg = nats[q]
             for h in range(2):
                 tp = bank(2 + 2 * (q % 3) + h, "wtp%d" % h)
                 srcs = []
@@ -110,21 +114,33 @@ def tile_ternarylineartorch_kernel(tc, x, weight, bias, gamma, out):
                         col = 256 * gg + 128 * u
                         srcs.append(words[:, col : col + 128])
                 four_transposes(tp, srcs)
-                copy_out(h == 1 and (q % 2 == 1 or q >= NQ - 2), tp, w_t[q][:, 512 * h : 512 * h + 512].bitcast(F32))
+                copy_out(h == 1 and q >= NQ - 1, tp, w_t[q][:, 512 * h : 512 * h + 512].bitcast(F32))
 
         def w_abs(q):
             nc.vector.tensor_scalar(
                 out=a_t[q][:], in0=w_t[q][:], scalar1=ABS_MASK, scalar2=None, op0=ALU.bitwise_and
             )
 
+        def w_vsum(q):
+            nc.vector.tensor_scalar(
+                out=junk[:],
+                in0=a_t[q][:].bitcast(BF16)[:, 0 : 128 * VSH],
+                scalar1=1.0,
+                scalar2=None,
+                op0=ALU.mult,
+                op1=ALU.add,
+                accum_out=vs[:, q : q + 1],
+            )
+
         def w_sums(q):
             cols = a_t[q][:].bitcast(BF16)
-            for j in range(16):
+            first = VSH if q < NQ - 1 else 0
+            for j in range(first, 16):
                 nc.tensor.matmul(
                     out=ssum_ps[:, 0:NSUM],
                     lhsT=cols[:, 128 * j : 128 * j + 128],
                     rhs=ones_bf[:],
-                    start=(q == 0 and j == 0),
+                    start=(q == 0 and j == first),
                     stop=(q == NQ - 1 and j == 15),
                 )
 
@@ -295,15 +311,24 @@ def tile_ternarylineartorch_kernel(tc, x, weight, bias, gamma, out):
                 event(e)
 
         with tc.tile_pool(name="stage", bufs=5) as stage:
-            for d in range(NQ // 2):
-                c, gp = divmod(d, 2)
-                nat = stage.tile([P, 4, 1024], BF16, name="wn", tag="nat")
-                rows = weight[512 * c : 512 * c + 512, 1024 * gp : 1024 * gp + 1024]
-                nc.sync.dma_start(out=nat[:], in_=rows.rearrange("(b p) k -> p b k", p=P))
-                nats[d] = nat
-                for q in (2 * d, 2 * d + 1):
+            for q in range(NQ):
+                c, g = divmod(q, G)
+                if q < NQ - 2 * 1:
+                    if q % 2 == 0:
+                        nat = stage.tile([P, 4, 1024], BF16, name="wn", tag="nat")
+                        rows = weight[512 * c : 512 * c + 512, 512 * g : 512 * g + 1024]
+                        nc.sync.dma_start(out=nat[:], in_=rows.rearrange("(b p) k -> p b k", p=P))
+                        nats[q] = (nat, 0)
+                        nats[q + 1] = (nat, 1)
+                else:
+                    nat = stage.tile([P, 4, 512], BF16, name="wl", tag="nat")
+                    rows = weight[512 * c : 512 * c + 512, 512 * g : 512 * g + 512]
+                    nc.sync.dma_start(out=nat[:], in_=rows.rearrange("(b p) k -> p b k", p=P))
+                    nats[q] = (nat, 0)
+                for q in [q]:
                     if q >= 1:
                         w_abs(q - 1)
+                        w_vsum(q - 1)
                     w_unit(q)
                     if q == 0:
                         nc.vector.tensor_copy(out=gam_f[:], in_=gam_bf[:])
@@ -321,12 +346,15 @@ def tile_ternarylineartorch_kernel(tc, x, weight, bias, gamma, out):
                 xnats[ip] = nat
             nc.sync.dma_start(out=bias_bc[:], in_=bias.partition_broadcast(P))
             w_abs(NQ - 1)
+            nc.vector.tensor_reduce(out=vsum[:], in_=vs[:], axis=mybir.AxisListType.X, op=ALU.add)
             for q in range(NQ - 3, NQ):
                 if q == NQ - 1:
                     for i in range(0):
                         x_tile(i)
                 w_sums(q)
-            nc.vector.tensor_copy(out=ssum_sb[:], in_=ssum_ps[:, 0:NSUM])
+            nc.vector.tensor_scalar(
+                out=ssum_sb[:], in0=ssum_ps[:, 0:NSUM], scalar1=vsum[:, 0:1], scalar2=None, op0=ALU.add
+            )
             th2_ps = bank(1, "th2_ps")
             nc.tensor.matmul(out=th2_ps[:, 0:NSUM], lhsT=ones_f[:], rhs=ssum_sb[:], start=True, stop=True)
             nc.vector.tensor_scalar(

@@ -21,7 +21,6 @@ NC = N // 512
 NQ = NC * G
 ABS_MASK = 0x7FFF7FFF
 SIGN_MASK = -0x7FFF8000
-VSH = 7
 NSUM = 32
 EV = {0: [("xq", 0), ("xq", 1), ("xq", 2), ("xq", 3), ("ps", 0, 0, 0), ("xt", 4), ("xt", 5), ("xt", 6), ("xt", 7)],
       1: [("ps", 0, 0, 1)],
@@ -69,10 +68,6 @@ def tile_ternarylineartorch_kernel(tc, x, weight, bias, gamma, out):
         nc.scalar.dma_start(out=brow_bf[0:16, :], in_=bias.rearrange("(b p) -> b p", p=P))
         brow_f = const.tile([P, P], F32, name="brow_f")
         bias_col = const.tile([P, 16], F32, name="bias_col")
-        vs = const.tile([P, NQ], F32, name="vs")
-        nc.vector.memset(vs[:], 0.0)
-        vsum = const.tile([P, 1], F32, name="vsum")
-        junk = const.tile([P, 128 * VSH], BF16, name="junk")
         ssum_sb = const.tile([P, NSUM], F32, name="ssum_sb")
         t_sb = const.tile([P, 1], F32, name="t_sb")
         bias_bc = const.tile([P, N], BF16, name="bias_bc")
@@ -104,7 +99,8 @@ def tile_ternarylineartorch_kernel(tc, x, weight, bias, gamma, out):
         xgs = {}
 
         def w_unit(q):
-            nat, gg = nats[q]
+            nat = nats[q // 2]
+            gg = q % 2
             for h in range(2):
                 tp = bank(2 + 2 * (q % 3) + h, "wtp%d" % h)
                 srcs = []
@@ -114,33 +110,21 @@ def tile_ternarylineartorch_kernel(tc, x, weight, bias, gamma, out):
                         col = 256 * gg + 128 * u
                         srcs.append(words[:, col : col + 128])
                 four_transposes(tp, srcs)
-                copy_out(h == 1 and q >= NQ - 1, tp, w_t[q][:, 512 * h : 512 * h + 512].bitcast(F32))
+                copy_out(h == 1 and (q % 2 == 1 or q >= NQ - 2), tp, w_t[q][:, 512 * h : 512 * h + 512].bitcast(F32))
 
         def w_abs(q):
             nc.vector.tensor_scalar(
                 out=a_t[q][:], in0=w_t[q][:], scalar1=ABS_MASK, scalar2=None, op0=ALU.bitwise_and
             )
 
-        def w_vsum(q):
-            nc.vector.tensor_scalar(
-                out=junk[:],
-                in0=a_t[q][:].bitcast(BF16)[:, 0 : 128 * VSH],
-                scalar1=1.0,
-                scalar2=None,
-                op0=ALU.mult,
-                op1=ALU.add,
-                accum_out=vs[:, q : q + 1],
-            )
-
         def w_sums(q):
             cols = a_t[q][:].bitcast(BF16)
-            first = VSH if q < NQ - 1 else 0
-            for j in range(first, 16):
+            for j in range(16):
                 nc.tensor.matmul(
                     out=ssum_ps[:, 0:NSUM],
                     lhsT=cols[:, 128 * j : 128 * j + 128],
                     rhs=ones_bf[:],
-                    start=(q == 0 and j == first),
+                    start=(q == 0 and j == 0),
                     stop=(q == NQ - 1 and j == 15),
                 )
 
@@ -311,31 +295,22 @@ def tile_ternarylineartorch_kernel(tc, x, weight, bias, gamma, out):
                 event(e)
 
         with tc.tile_pool(name="stage", bufs=5) as stage:
-            for q in range(NQ):
-                c, g = divmod(q, G)
-                if q < NQ - 2 * 1:
-                    if q % 2 == 0:
-                        nat = stage.tile([P, 4, 1024], BF16, name="wn", tag="nat")
-                        rows = weight[512 * c : 512 * c + 512, 512 * g : 512 * g + 1024]
-                        nc.sync.dma_start(out=nat[:], in_=rows.rearrange("(b p) k -> p b k", p=P))
-                        nats[q] = (nat, 0)
-                        nats[q + 1] = (nat, 1)
-                else:
-                    nat = stage.tile([P, 4, 512], BF16, name="wl", tag="nat")
-                    rows = weight[512 * c : 512 * c + 512, 512 * g : 512 * g + 512]
-                    nc.sync.dma_start(out=nat[:], in_=rows.rearrange("(b p) k -> p b k", p=P))
-                    nats[q] = (nat, 0)
-                for q in [q]:
+            for d in range(NQ // 2):
+                c, gp = divmod(d, 2)
+                nat = stage.tile([P, 4, 1024], BF16, name="wn", tag="nat")
+                rows = weight[512 * c : 512 * c + 512, 1024 * gp : 1024 * gp + 1024]
+                nc.sync.dma_start(out=nat[:], in_=rows.rearrange("(b p) k -> p b k", p=P))
+                nats[d] = nat
+                for q in (2 * d, 2 * d + 1):
                     if q >= 1:
                         w_abs(q - 1)
-                        w_vsum(q - 1)
                     w_unit(q)
-                    if q == 0:
+                    if q == 9:
                         nc.vector.tensor_copy(out=gam_f[:], in_=gam_bf[:])
                         nc.vector.tensor_copy(out=brow_f[:], in_=brow_bf[:])
                     if q >= 3:
                         w_sums(q - 3)
-                    if q == 2:
+                    if q == 11:
                         nc.tensor.transpose(th_ps[:, 0:128], brow_f[:], ident[:])
                         nc.vector.tensor_copy(out=bias_col[:], in_=th_ps[:, 0:16])
             for ip in range(MT // 2):
@@ -346,15 +321,12 @@ def tile_ternarylineartorch_kernel(tc, x, weight, bias, gamma, out):
                 xnats[ip] = nat
             nc.sync.dma_start(out=bias_bc[:], in_=bias.partition_broadcast(P))
             w_abs(NQ - 1)
-            nc.vector.tensor_reduce(out=vsum[:], in_=vs[:], axis=mybir.AxisListType.X, op=ALU.add)
             for q in range(NQ - 3, NQ):
                 if q == NQ - 1:
                     for i in range(0):
                         x_tile(i)
                 w_sums(q)
-            nc.vector.tensor_scalar(
-                out=ssum_sb[:], in0=ssum_ps[:, 0:NSUM], scalar1=vsum[:, 0:1], scalar2=None, op0=ALU.add
-            )
+            nc.vector.tensor_copy(out=ssum_sb[:], in_=ssum_ps[:, 0:NSUM])
             th2_ps = bank(1, "th2_ps")
             nc.tensor.matmul(out=th2_ps[:, 0:NSUM], lhsT=ones_f[:], rhs=ssum_sb[:], start=True, stop=True)
             nc.vector.tensor_scalar(

@@ -45,7 +45,6 @@ PRE = []
 def tile_ternarylineartorch_kernel(tc, x, weight, bias, gamma, out):
     nc = tc.nc
     with ExitStack() as ctx:
-        ctx.enter_context(tc.manual_schedule())
         const = ctx.enter_context(tc.tile_pool(name="const", bufs=1))
         keep = ctx.enter_context(tc.tile_pool(name="keep", bufs=1))
         xgp = ctx.enter_context(tc.tile_pool(name="xgp", bufs=4))
@@ -305,12 +304,12 @@ def tile_ternarylineartorch_kernel(tc, x, weight, bias, gamma, out):
                     if q >= 1:
                         w_abs(q - 1)
                     w_unit(q)
-                    if q == 9:
+                    if q == 0:
                         nc.vector.tensor_copy(out=gam_f[:], in_=gam_bf[:])
                         nc.vector.tensor_copy(out=brow_f[:], in_=brow_bf[:])
                     if q >= 3:
                         w_sums(q - 3)
-                    if q == 11:
+                    if q == 2:
                         nc.tensor.transpose(th_ps[:, 0:128], brow_f[:], ident[:])
                         nc.vector.tensor_copy(out=bias_col[:], in_=th_ps[:, 0:16])
             for ip in range(MT // 2):

@@ -15,31 +15,13 @@ ACT = mybir.ActivationFunctionType
 P = 128
 M, K, N = 1024, 2048, 2048
 FLOPS = 2 * M * K * N
-G = K // 512
-MT = M // P
-NC = N // 512
-NQ = NC * G
 ABS_MASK = 0x7FFF7FFF
 SIGN_MASK = -0x7FFF8000
 NSUM = 32
-EV = {0: [("xq", 0), ("xq", 1), ("xq", 2), ("xq", 3), ("ps", 0, 0, 0), ("xt", 4), ("xt", 5), ("xt", 6), ("xt", 7)],
-      1: [("ps", 0, 0, 1)],
-      2: [("xq", 4), ("xq", 5), ("xq", 6), ("xq", 7), ("ps", 0, 0, 2), ("pv", 0, 1, 0), ("pv", 0, 1, 1), ("pv", 0, 1, 2)],
-      3: [("ps", 0, 0, 3), ("s1", 0, 0), ("pv", 0, 1, 3)],
-      4: [("ea", 0, 1), ("bt", 0, 0), ("s2", 0, 0), ("pv", 1, 1, 0), ("eg", 0, 1), ("ps", 1, 0, 0)],
-      5: [("ps", 1, 0, 1), ("pv", 1, 1, 1)],
-      6: [("ps", 1, 0, 2), ("pv", 1, 1, 2)],
-      7: [("ps", 1, 0, 3), ("s1", 1, 0), ("pv", 1, 1, 3)],
-      8: [("ea", 1, 1), ("bt", 1, 0), ("s2", 1, 0), ("pv", 2, 1, 0), ("eg", 1, 1), ("ps", 2, 0, 0)],
-      9: [("ps", 2, 0, 1), ("pv", 2, 1, 1)],
-      10: [("ps", 2, 0, 2), ("pv", 2, 1, 2)],
-      11: [("ps", 2, 0, 3), ("s1", 2, 0), ("pv", 2, 1, 3)],
-      12: [("ea", 2, 1), ("bt", 2, 0), ("s2", 2, 0), ("pv", 3, 1, 0), ("eg", 2, 1), ("pv", 3, 0, 0)],
-      13: [("pv", 3, 0, 1), ("pv", 3, 1, 1)],
-      14: [("pv", 3, 0, 2), ("pv", 3, 1, 2)],
-      15: [("pv", 3, 0, 3), ("pv", 3, 1, 3)],
-      16: [("el", 3, 0), ("el", 3, 1)]}
-PRE = []
+ND = N // 256
+NQ = 2 * ND
+S_FULL = 4
+S_HALF = 6
 
 
 def tile_ternarylineartorch_kernel(tc, x, weight, bias, gamma, out):
@@ -47,39 +29,77 @@ def tile_ternarylineartorch_kernel(tc, x, weight, bias, gamma, out):
     with ExitStack() as ctx:
         const = ctx.enter_context(tc.tile_pool(name="const", bufs=1))
         keep = ctx.enter_context(tc.tile_pool(name="keep", bufs=1))
-        xgp = ctx.enter_context(tc.tile_pool(name="xgp", bufs=4))
+        xgp = ctx.enter_context(tc.tile_pool(name="xgp", bufs=2))
+        yp = ctx.enter_context(tc.tile_pool(name="yp", bufs=3))
         psum = ctx.enter_context(tc.psum_pool(name="psum", bufs=1))
 
         def bank(k, name):
             return psum.tile([P, 512], F32, tag="b%d" % k, name=name)
 
+        gam_bf = const.tile([P, 1], BF16, name="gam_bf")
+        nc.sync.dma_start(out=gam_bf[:], in_=gamma.partition_broadcast(P))
+        brow_bf = const.tile([P, P], BF16, name="brow_bf")
+        nc.vector.memset(brow_bf[:], 0.0)
+        nc.sync.dma_start(out=brow_bf[0:16, :], in_=bias.rearrange("(b p) -> b p", p=P))
+        brow1 = keep.tile([P, N], BF16, name="brow1", tag="w_t15", align_bytes=64)
+        nc.vector.memset(brow1[:], 0.0)
+        nc.sync.dma_start(out=brow1[0:1, :], in_=bias.unsqueeze(0))
         ident = const.tile([P, P], F32, name="ident")
         make_identity(nc, ident[:])
-        ones_bf = const.tile([P, NSUM], BF16, name="ones_bf")
+        ones_bf = const.tile([P, P], BF16, name="ones_bf")
         nc.vector.memset(ones_bf[:], 1.0)
         ones_f = const.tile([P, P], F32, name="ones_f")
         nc.vector.memset(ones_f[:], 1.0)
-        gam_bf = const.tile([P, 1], BF16, name="gam_bf")
-        nc.scalar.dma_start(out=gam_bf[:], in_=gamma.partition_broadcast(P))
         gam_f = const.tile([P, 1], F32, name="gam_f")
-        brow_bf = const.tile([P, P], BF16, name="brow_bf")
-        nc.vector.memset(brow_bf[:], 0.0)
-        nc.scalar.dma_start(out=brow_bf[0:16, :], in_=bias.rearrange("(b p) -> b p", p=P))
         brow_f = const.tile([P, P], F32, name="brow_f")
         bias_col = const.tile([P, 16], F32, name="bias_col")
         ssum_sb = const.tile([P, NSUM], F32, name="ssum_sb")
         t_sb = const.tile([P, 1], F32, name="t_sb")
         bias_bc = const.tile([P, N], BF16, name="bias_bc")
 
-        w_t = [keep.tile([P, 1024], I32, name="w_t%d" % q, align_bytes=64) for q in range(NQ)]
-        a_t = [keep.tile([P, 1024], I32, name="a_t%d" % q, align_bytes=64) for q in range(NQ)]
-        w_codes = [keep.tile([P, 512], U32, name="w_codes%d" % q, align_bytes=64) for q in range(4)]
+        for c in range(4):
+            bb = bank(2 + c, "bb")
+            nc.tensor.matmul(
+                out=bb[:], lhsT=ones_bf[:], rhs=brow1[:, 512 * c : 512 * c + 512], start=True, stop=True
+            )
+            nc.scalar.copy(out=bias_bc[:, 512 * c : 512 * c + 512], in_=bb[:])
+
+        w_t = [None] * NQ
+        a_t = [None] * NQ
         w_sc = [keep.tile([P, 512], U8, name="w_sc%d" % q, align_bytes=64) for q in range(NQ)]
-        x_codes = [keep.tile([P, G, 512], U32, name="x_codes%d" % h, align_bytes=64) for h in range(2)]
-        x_sc = [keep.tile([P, G, 512], U8, name="x_sc%d" % h, align_bytes=64) for h in range(2)]
+        x_codes = [keep.tile([P, 4, 512], U32, name="x_codes%d" % h, align_bytes=64) for h in range(2)]
+        x_sc = [keep.tile([P, 4, 512], U8, name="x_sc%d" % h, align_bytes=64) for h in range(2)]
 
         ssum_ps = bank(0, "ssum_ps")
         th_ps = bank(1, "th_ps")
+
+        slot = [0]
+
+        def stage(shape, name):
+            t = keep.tile(shape, BF16, name=name, tag="nat%d" % (slot[0] % 5), align_bytes=64)
+            slot[0] += 1
+            return t
+
+        nats = {}
+
+        def load_w(d):
+            nat = stage([P, 2, K], "wn")
+            nc.sync.dma_start(out=nat[:], in_=weight[256 * d : 256 * d + 256, :].rearrange("(b p) k -> p b k", p=P))
+            for gg in range(2):
+                nats[2 * d + gg] = (nat, 512 * gg)
+
+        def load_w_half(d, gg):
+            nat = stage([P, 2, K // 2], "wh")
+            src = weight[256 * d : 256 * d + 256, 1024 * gg : 1024 * gg + 1024]
+            nc.sync.dma_start(out=nat[:], in_=src.rearrange("(b p) k -> p b k", p=P))
+            nats[2 * d + gg] = (nat, 0)
+
+        xnats = {}
+
+        def load_x(ip):
+            nat = stage([P, 2, K], "xn")
+            nc.sync.dma_start(out=nat[:], in_=x[256 * ip : 256 * ip + 256, :].rearrange("(b p) k -> p b k", p=P))
+            xnats[ip] = nat
 
         def four_transposes(tp, sources):
             for j in range(4):
@@ -93,27 +113,36 @@ def tile_ternarylineartorch_kernel(tc, x, weight, bias, gamma, out):
             else:
                 nc.scalar.copy(out=dst, in_=src)
 
-        nats = {}
-        xnats = {}
-        xgs = {}
-
         def w_unit(q):
-            nat = nats[q // 2]
-            gg = q % 2
-            for h in range(2):
-                tp = bank(2 + 2 * (q % 3) + h, "wtp%d" % h)
+            nat, base = nats[q]
+            w_t[q] = keep.tile([P, 1024], I32, name="w_t", tag="w_t%d" % q, align_bytes=64)
+            for gi in range(2):
+                tp = bank(2 + (2 * q + gi) % 6, "wtp")
                 srcs = []
-                for bl in range(2):
-                    words = nat[:, 2 * h + bl, :].bitcast(F32)
+                for b in range(2):
+                    words = nat[:, b, :].bitcast(F32)
                     for u in range(2):
-                        col = 256 * gg + 128 * u
+                        col = base + 256 * gi + 128 * u
                         srcs.append(words[:, col : col + 128])
                 four_transposes(tp, srcs)
-                copy_out(h == 1 and (q % 2 == 1 or q >= NQ - 2), tp, w_t[q][:, 512 * h : 512 * h + 512].bitcast(F32))
+                copy_out(gi == 1 and (q % 2 == 1 or q >= NQ - 2), tp, w_t[q][:, 512 * gi : 512 * gi + 512].bitcast(F32))
+
+        def new_a(q):
+            a_t[q] = keep.tile([P, 1024], I32, name="a_t", tag="a_t%d" % q, align_bytes=64)
 
         def w_abs(q):
             nc.vector.tensor_scalar(
                 out=a_t[q][:], in0=w_t[q][:], scalar1=ABS_MASK, scalar2=None, op0=ALU.bitwise_and
+            )
+
+        def nat_abs(q):
+            nat = nats[q][0]
+            nc.vector.tensor_scalar(
+                out=a_t[q][:],
+                in0=nat[:].rearrange("p b k -> p (b k)").bitcast(I32),
+                scalar1=ABS_MASK,
+                scalar2=None,
+                op0=ALU.bitwise_and,
             )
 
         def w_sums(q):
@@ -122,27 +151,34 @@ def tile_ternarylineartorch_kernel(tc, x, weight, bias, gamma, out):
                 nc.tensor.matmul(
                     out=ssum_ps[:, 0:NSUM],
                     lhsT=cols[:, 128 * j : 128 * j + 128],
-                    rhs=ones_bf[:],
+                    rhs=ones_bf[:, 0:NSUM],
                     start=(q == 0 and j == 0),
                     stop=(q == NQ - 1 and j == 15),
                 )
 
-        def x_tile(i):
-            words = xnats[i // 2][:, i % 2, :].bitcast(F32)
-            xg = xgp.tile([P, 1024], F32, name="xg", align_bytes=64)
-            for h in range(2):
-                tp = bank(4 + 2 * (i % 2) + h, "xtp%d" % h)
-                four_transposes(tp, [words[:, 512 * h + 128 * j : 512 * h + 128 * j + 128] for j in range(4)])
-                copy_out(False, tp, xg[:, 512 * h : 512 * h + 512])
-            xgs[i] = xg
+        xgs = {}
 
-        def x_quant(i):
-            h, j = divmod(i, 4)
-            for g in range(G):
+        def x_pair(ip, banks):
+            xg = xgp.tile([P, 4, 512], F32, name="xg", align_bytes=64)
+            for g in range(4):
+                tp = bank(banks[g], "xtp")
+                srcs = []
+                for b in range(2):
+                    words = xnats[ip][:, b, :].bitcast(F32)
+                    for u in range(2):
+                        col = 256 * g + 128 * u
+                        srcs.append(words[:, col : col + 128])
+                four_transposes(tp, srcs)
+                copy_out(False, tp, xg[:, g, :])
+            xgs[ip] = xg
+
+        def x_quant(ip):
+            h, t = divmod(ip, 2)
+            for g in range(4):
                 nc.vector.quantize_mx(
-                    out=x_codes[h][:, g, P * j : P * j + P].bitcast(FP8X4),
-                    scales=x_sc[h][:, g, P * j : P * j + P],
-                    in_=xgs[i][:, 256 * g : 256 * g + 256].bitcast(BF16),
+                    out=x_codes[h][:, g, 256 * t : 256 * t + 256].bitcast(FP8X4),
+                    scales=x_sc[h][:, g, 256 * t : 256 * t + 256],
+                    in_=xgs[ip][:, g, :].bitcast(BF16),
                 )
 
         def mask(q):
@@ -159,189 +195,246 @@ def tile_ternarylineartorch_kernel(tc, x, weight, bias, gamma, out):
                 op1=ALU.bitwise_or,
             )
 
+        w_codes = {}
+
         def w_quant(q):
-            nc.vector.quantize_mx(
-                out=w_codes[q][:].bitcast(FP8X4), scales=w_sc[q][:], in_=a_t[q][:].bitcast(BF16)
-            )
+            codes = keep.tile([P, 512], U32, name="w_codes", tag="w_t%d" % q, align_bytes=64)
+            nc.vector.quantize_mx(out=codes[:].bitcast(FP8X4), scales=w_sc[q][:], in_=a_t[q][:].bitcast(BF16))
+            w_codes[q] = codes
+
+        def transposed(d, h):
+            return d < S_FULL or (d < S_HALF and h == 0)
 
         accs = {}
 
-        def passes(c, h, g, route):
-            q = G * c + g
-            for j in range(4):
-                if g == 0:
-                    accs[(c, h, j)] = bank(4 * h + j, "acc")
-                if route == "V":
+        def passes_s(q, h):
+            d, gg = divmod(q, 2)
+            for j in range(2):
+                if gg == 0:
+                    accs[(d, h, j)] = bank(4 * (d % 2) + 2 * h + j, "acc_s")
+                for gi in range(2):
+                    g = 2 * gg + gi
+                    c0 = 256 * gi + 128 * j
                     nc.tensor.matmul_mx(
-                        out=accs[(c, h, j)][:],
-                        lhsT=x_codes[h][:, g, P * j : P * j + P].bitcast(FP8X4),
-                        lhsT_scale=x_sc[h][:, g, P * j : P * j + P],
-                        rhs=w_codes[q][:].bitcast(FP8X4),
-                        rhs_scale=w_sc[q][:],
-                        start=(g == 0),
-                        stop=(g == G - 1),
-                    )
-                else:
-                    nc.tensor.matmul_mx(
-                        out=accs[(c, h, j)][:],
-                        lhsT=w_codes[q][:, P * j : P * j + P].bitcast(FP8X4),
-                        lhsT_scale=w_sc[q][:, P * j : P * j + P],
+                        out=accs[(d, h, j)][:],
+                        lhsT=w_codes[q][:, c0 : c0 + 128].bitcast(FP8X4),
+                        lhsT_scale=w_sc[q][:, c0 : c0 + 128],
                         rhs=x_codes[h][:, g, :].bitcast(FP8X4),
                         rhs_scale=x_sc[h][:, g, :],
                         start=(g == 0),
-                        stop=(g == G - 1),
+                        stop=(g == 3),
                     )
 
-        def store(c, h, jp, o):
-            r0 = 512 * h + 256 * jp
-            nc.sync.dma_start(
-                out=out[r0 : r0 + 256, 512 * c : 512 * c + 512].rearrange("(t p) n -> p t n", p=P), in_=o[:]
+        def pass_v(dst, d, h, j, g):
+            q, gi = 2 * d + g // 2, g % 2
+            nc.tensor.matmul_mx(
+                out=dst,
+                lhsT=x_codes[h][:, g, P * j : P * j + P].bitcast(FP8X4),
+                lhsT_scale=x_sc[h][:, g, P * j : P * j + P],
+                rhs=w_codes[q][:, 256 * gi : 256 * gi + 256].bitcast(FP8X4),
+                rhs_scale=w_sc[q][:, 256 * gi : 256 * gi + 256],
+                start=(g == 0),
+                stop=(g == 3),
             )
+
+        def passes_v(d, h):
+            for b in range(2):
+                acc = bank(4 * (d % 2) + 2 * h + b, "acc_v")
+                for t in range(2):
+                    for g in range(4):
+                        pass_v(acc[:, 256 * t : 256 * t + 256], d, h, 2 * b + t, g)
+                accs[(d, h, b)] = acc
+
+        def passes_last(gg, tiles):
+            d = ND - 1
+            for i in tiles:
+                if gg == 0:
+                    accs[(d, i)] = bank((4 + i) % 8, "acc_l")
+                for gi in range(2):
+                    pass_v(accs[(d, i)][:, 0:256], d, i // 4, i % 4, 2 * gg + gi)
+
+        def rows(r0, nrows, d):
+            return out[r0 : r0 + nrows, 256 * d : 256 * d + 256].rearrange("(t p) n -> p t n", p=P)
+
+        def new_o(d, h):
+            return keep.tile([P, 2, 512], F32, name="o", tag="a_t%d" % (2 * d + h), align_bytes=64)
 
         ovs = {}
 
-        def epilogue_add(c, h):
-            for jp in range(2):
-                o = keep.tile([P, 2, 512], F32, name="ov", tag="w_t%d" % (2 * h + jp), align_bytes=64)
+        def add_v(d, h):
+            o = new_o(d, h)
+            bcast = bias_bc[:, 256 * d : 256 * d + 256].unsqueeze(1).to_broadcast([P, 2, 256])
+            for b in range(2):
+                nc.vector.tensor_tensor(
+                    out=o[:, b, :].rearrange("p (t n) -> p t n", t=2),
+                    in0=accs[(d, h, b)][:].rearrange("p (t n) -> p t n", t=2),
+                    in1=bcast,
+                    op=ALU.add,
+                )
+            ovs[(d, h)] = o
+
+        def gain_v(d, h):
+            o = ovs[(d, h)]
+            for b in range(2):
+                nc.scalar.activation(out=o[:, b, :], in_=o[:, b, :], func=ACT.Copy, scale=gam_f[:, 0:1])
+                nc.sync.dma_start(
+                    out=rows(512 * h + 256 * b, 256, d), in_=o[:, b, :].rearrange("p (t n) -> p t n", t=2)
+                )
+
+        def last(h):
+            d = ND - 1
+            o = new_o(d, h)
+            for b in range(2):
                 for t in range(2):
                     nc.vector.tensor_tensor(
-                        out=o[:, t, :],
-                        in0=accs[(c, h, 2 * jp + t)][:],
-                        in1=bias_bc[:, 512 * c : 512 * c + 512],
+                        out=o[:, b, 256 * t : 256 * t + 256],
+                        in0=accs[(d, 4 * h + 2 * b + t)][:, 0:256],
+                        in1=bias_bc[:, 256 * d : 256 * d + 256],
                         op=ALU.add,
                     )
-                ovs[(c, h, jp)] = o
-
-        def epilogue_gain(c, h):
-            for jp in range(2):
-                o = ovs[(c, h, jp)]
-                nc.scalar.activation(out=o[:], in_=o[:], func=ACT.Copy, scale=gam_f[:, 0:1])
-                store(c, h, jp, o)
-
-        def epilogue_last(c, h):
-            for j in range(4):
-                i = 4 * h + j
-                o = keep.tile([P, 512], F32, name="ol", tag="%s_t%d" % ("wa"[h], 4 + j), align_bytes=64)
-                nc.vector.tensor_tensor(
-                    out=o[:], in0=accs[(c, h, j)][:], in1=bias_bc[:, 512 * c : 512 * c + 512], op=ALU.add
+                nc.scalar.activation(out=o[:, b, :], in_=o[:, b, :], func=ACT.Copy, scale=gam_f[:, 0:1])
+                nc.sync.dma_start(
+                    out=rows(512 * h + 256 * b, 256, d), in_=o[:, b, :].rearrange("p (t n) -> p t n", t=2)
                 )
-                nc.scalar.activation(out=o[:], in_=o[:], func=ACT.Copy, scale=gam_f[:, 0:1])
-                nc.sync.dma_start(out=out[P * i : P * i + P, 512 * c : 512 * c + 512], in_=o[:])
 
         ys = {}
 
-        def s_first(c, h):
-            for jp in range(2):
-                y = keep.tile([P, 2, 512], F32, name="y", tag="a_t%d" % (2 * h + jp), align_bytes=64)
-                for t in range(2):
-                    nb = 4 * c + 2 * jp + t
-                    nc.scalar.activation(
-                        out=y[:, t, :],
-                        in_=accs[(c, h, 2 * jp + t)][:],
-                        func=ACT.Identity,
-                        bias=bias_col[:, nb : nb + 1],
-                        scale=1.0,
-                    )
-                ys[(c, h, jp)] = y
+        def s_first(d, h):
+            y = yp.tile([P, 2, 512], F32, name="y", align_bytes=64)
+            for j in range(2):
+                nb = 2 * d + j
+                nc.scalar.activation(
+                    out=y[:, j, :],
+                    in_=accs[(d, h, j)][:],
+                    func=ACT.Identity,
+                    bias=bias_col[:, nb : nb + 1],
+                    scale=1.0,
+                )
+            ys[(d, h)] = y
 
         backs = {}
 
-        def back(c, h):
-            for j in range(4):
-                bt = bank(4 * h + j, "bt")
-                four_transposes(bt, [ys[(c, h, nbl // 2)][:, nbl % 2, P * j : P * j + P] for nbl in range(4)])
-                backs[(c, h, j)] = bt
+        def back(d, h):
+            for b in range(2):
+                bt = bank(4 * (d % 2) + 2 * h + b, "bt")
+                y = ys[(d, h)]
+                four_transposes(bt, [y[:, j, 128 * (2 * b + t) : 128 * (2 * b + t) + 128] for t in range(2) for j in range(2)])
+                backs[(d, h, b)] = bt
 
-        def s_second(c, h):
-            for jp in range(2):
-                o = keep.tile([P, 2, 512], F32, name="os", tag="w_t%d" % (2 * h + jp), align_bytes=64)
-                for t in range(2):
-                    nc.scalar.activation(
-                        out=o[:, t, :], in_=backs[(c, h, 2 * jp + t)][:], func=ACT.Copy, scale=gam_f[:, 0:1]
-                    )
-                store(c, h, jp, o)
+        def s_second(d, h):
+            o = new_o(d, h)
+            for b in range(2):
+                nc.scalar.activation(out=o[:, b, :], in_=backs[(d, h, b)][:], func=ACT.Copy, scale=gam_f[:, 0:1])
+                nc.sync.dma_start(
+                    out=rows(512 * h + 256 * b, 256, d), in_=o[:, b, :].rearrange("p (t n) -> p t n", t=2)
+                )
 
+        for d in range(ND - 1):
+            load_w(d)
+            for q in (2 * d, 2 * d + 1):
+                if q >= 1:
+                    new_a(q - 1)
+                    w_abs(q - 1)
+                w_unit(q)
+                if q >= 3:
+                    w_sums(q - 3)
+                if q == 1:
+                    nc.vector.tensor_copy(out=gam_f[:], in_=gam_bf[:])
+                    nc.vector.tensor_copy(out=brow_f[:], in_=brow_bf[:])
+                if q == 3:
+                    nc.tensor.transpose(th_ps[:, 0:128], brow_f[:], ident[:])
+                    nc.vector.tensor_copy(out=bias_col[:], in_=th_ps[:, 0:16])
+        for gg in range(2):
+            load_w_half(ND - 1, gg)
+        for ip in range(4):
+            load_x(ip)
+        new_a(NQ - 3)
+        w_abs(NQ - 3)
+        w_sums(NQ - 5)
+        w_sums(NQ - 4)
+        new_a(NQ - 2)
+        nat_abs(NQ - 2)
+        w_sums(NQ - 3)
+        w_unit(NQ - 2)
+        w_sums(NQ - 2)
+        new_a(NQ - 1)
+        nat_abs(NQ - 1)
+        w_sums(NQ - 1)
+        nc.vector.tensor_copy(out=ssum_sb[:], in_=ssum_ps[:, 0:NSUM])
+        th2_ps = bank(1, "th2_ps")
+        nc.tensor.matmul(out=th2_ps[:, 0:NSUM], lhsT=ones_f[:], rhs=ssum_sb[:], start=True, stop=True)
+        nc.vector.tensor_scalar(out=t_sb[:], in0=th2_ps[:, 0:1], scalar1=0.5 / (N * K), scalar2=None, op0=ALU.mult)
+        mask(0)
+        w_unit(NQ - 1)
+        x_pair(0, (4, 5, 6, 7))
+        x_pair(1, (4, 5, 6, 7))
 
-        def event(e):
-            k = e[0]
-            if k == "xq":
-                x_quant(e[1])
-            elif k == "xt":
-                x_tile(e[1])
-            elif k == "pv":
-                passes(e[1], e[2], e[3], "V")
-            elif k == "ps":
-                passes(e[1], e[2], e[3], "S")
-            elif k == "s1":
-                s_first(e[1], e[2])
-            elif k == "bt":
-                back(e[1], e[2])
-            elif k == "s2":
-                s_second(e[1], e[2])
-            elif k == "ea":
-                epilogue_add(e[1], e[2])
-            elif k == "eg":
-                epilogue_gain(e[1], e[2])
-            elif k == "el":
-                epilogue_last(e[1], e[2])
-
-        def step(q):
+        for q in range(NQ):
+            d, gg = divmod(q, 2)
             signed(q)
             if q + 1 < NQ:
+                if q + 1 >= NQ - 2:
+                    w_abs(q + 1)
                 mask(q + 1)
             w_quant(q)
-            for e in EV.get(q, []):
-                event(e)
-
-        with tc.tile_pool(name="stage", bufs=5) as stage:
-            for d in range(NQ // 2):
-                c, gp = divmod(d, 2)
-                nat = stage.tile([P, 4, 1024], BF16, name="wn", tag="nat")
-                rows = weight[512 * c : 512 * c + 512, 1024 * gp : 1024 * gp + 1024]
-                nc.sync.dma_start(out=nat[:], in_=rows.rearrange("(b p) k -> p b k", p=P))
-                nats[d] = nat
-                for q in (2 * d, 2 * d + 1):
-                    if q >= 1:
-                        w_abs(q - 1)
-                    w_unit(q)
-                    if q == 0:
-                        nc.vector.tensor_copy(out=gam_f[:], in_=gam_bf[:])
-                        nc.vector.tensor_copy(out=brow_f[:], in_=brow_bf[:])
-                    if q >= 3:
-                        w_sums(q - 3)
-                    if q == 2:
-                        nc.tensor.transpose(th_ps[:, 0:128], brow_f[:], ident[:])
-                        nc.vector.tensor_copy(out=bias_col[:], in_=th_ps[:, 0:16])
-            for ip in range(MT // 2):
-                nat = stage.tile([P, 2, K], BF16, name="xn", tag="nat")
-                nc.sync.dma_start(
-                    out=nat[:], in_=x[256 * ip : 256 * ip + 256, :].rearrange("(t p) k -> p t k", p=P)
-                )
-                xnats[ip] = nat
-            nc.sync.dma_start(out=bias_bc[:], in_=bias.partition_broadcast(P))
-            w_abs(NQ - 1)
-            for q in range(NQ - 3, NQ):
-                if q == NQ - 1:
-                    for i in range(0):
-                        x_tile(i)
-                w_sums(q)
-            nc.vector.tensor_copy(out=ssum_sb[:], in_=ssum_ps[:, 0:NSUM])
-            th2_ps = bank(1, "th2_ps")
-            nc.tensor.matmul(out=th2_ps[:, 0:NSUM], lhsT=ones_f[:], rhs=ssum_sb[:], start=True, stop=True)
-            nc.vector.tensor_scalar(
-                out=t_sb[:], in0=th2_ps[:, 0:1], scalar1=0.5 / (N * K), scalar2=None, op0=ALU.mult
-            )
-            for i in range(0, 4):
-                x_tile(i)
-            mask(0)
-            for e in PRE:
-                event(e)
-            for q in range(2):
-                step(q)
-        codes = ctx.enter_context(tc.tile_pool(name="codes", bufs=1))
-        for q in range(4, NQ):
-            w_codes.append(codes.tile([P, 512], U32, name="w_codes%d" % q, align_bytes=64))
-        for q in range(2, NQ):
-            step(q)
-        for e in EV.get(NQ, []):
-            event(e)
+            if q == 0:
+                x_quant(0)
+                x_quant(1)
+                x_pair(2, (2, 3, 6, 7))
+                passes_s(0, 0)
+                x_pair(3, (2, 3, 6, 7))
+                continue
+            if q == 1:
+                x_quant(2)
+                passes_s(1, 0)
+                s_first(0, 0)
+                continue
+            if q == 2:
+                passes_s(2, 0)
+                x_quant(3)
+                back(0, 0)
+                s_second(0, 0)
+                for qq in (0, 1):
+                    passes_s(qq, 1)
+                s_first(0, 1)
+                passes_s(2, 1)
+                continue
+            if q == 3:
+                passes_s(3, 0)
+                s_first(1, 0)
+                back(0, 1)
+                s_second(0, 1)
+                passes_s(3, 1)
+                s_first(1, 1)
+                continue
+            if gg == 0:
+                if d - 1 >= 0 and not transposed(d - 1, 0):
+                    add_v(d - 1, 0)
+                    gain_v(d - 1, 0)
+            else:
+                if d - 1 >= 0 and not transposed(d - 1, 1):
+                    add_v(d - 1, 1)
+                    gain_v(d - 1, 1)
+            if d == ND - 1:
+                if gg == 0:
+                    passes_last(0, range(6))
+                else:
+                    passes_last(0, range(6, 8))
+                    passes_last(1, range(8))
+            else:
+                for h in range(2):
+                    if transposed(d, h):
+                        passes_s(q, h)
+                    elif gg == 1:
+                        passes_v(d, h)
+            if d < ND - 1 and gg == 1:
+                for h in range(2):
+                    if transposed(d, h):
+                        s_first(d, h)
+            if gg == 0:
+                for h in range(2):
+                    if transposed(d - 1, h):
+                        back(d - 1, h)
+                        s_second(d - 1, h)
+        for h in range(2):
+            last(h)

@@ -32,6 +32,7 @@ def tile_ternarylineartorch_kernel(tc, x, weight, bias, gamma, out):
         xgp = ctx.enter_context(tc.tile_pool(name="xgp", bufs=2))
         yp = ctx.enter_context(tc.tile_pool(name="yp", bufs=3))
         psum = ctx.enter_context(tc.psum_pool(name="psum", bufs=1))
+        ctx.enter_context(tc.manual_schedule())
 
         def bank(k, name):
             return psum.tile([P, 512], F32, tag="b%d" % k, name=name)
@@ -88,11 +89,12 @@ def tile_ternarylineartorch_kernel(tc, x, weight, bias, gamma, out):
             for gg in range(2):
                 nats[2 * d + gg] = (nat, 512 * gg)
 
-        def load_w_half(d, gg):
-            nat = stage([P, 2, K // 2], "wh")
-            src = weight[256 * d : 256 * d + 256, 1024 * gg : 1024 * gg + 1024]
-            nc.sync.dma_start(out=nat[:], in_=src.rearrange("(b p) k -> p b k", p=P))
-            nats[2 * d + gg] = (nat, 0)
+        def load_w_halves(d):
+            nat = stage([P, 2, 2, K // 2], "wh")
+            for gg in range(2):
+                src = weight[256 * d : 256 * d + 256, 1024 * gg : 1024 * gg + 1024]
+                nc.sync.dma_start(out=nat[:, gg, :, :], in_=src.rearrange("(b p) k -> p b k", p=P))
+                nats[2 * d + gg] = (nat[:, gg, :, :], 0)
 
         xnats = {}
 
@@ -113,11 +115,11 @@ def tile_ternarylineartorch_kernel(tc, x, weight, bias, gamma, out):
             else:
                 nc.scalar.copy(out=dst, in_=src)
 
-        def w_unit(q):
+        def w_unit(q, banks=None):
             nat, base = nats[q]
             w_t[q] = keep.tile([P, 1024], I32, name="w_t", tag="w_t%d" % q, align_bytes=64)
             for gi in range(2):
-                tp = bank(2 + (2 * q + gi) % 6, "wtp")
+                tp = bank(banks[gi] if banks else 2 + (2 * q + gi) % 6, "wtp")
                 srcs = []
                 for b in range(2):
                     words = nat[:, b, :].bitcast(F32)
@@ -125,7 +127,7 @@ def tile_ternarylineartorch_kernel(tc, x, weight, bias, gamma, out):
                         col = base + 256 * gi + 128 * u
                         srcs.append(words[:, col : col + 128])
                 four_transposes(tp, srcs)
-                copy_out(gi == 1 and (q % 2 == 1 or q >= NQ - 2), tp, w_t[q][:, 512 * gi : 512 * gi + 512].bitcast(F32))
+                copy_out(gi == 1 and q % 2 == 1 and q < 12, tp, w_t[q][:, 512 * gi : 512 * gi + 512].bitcast(F32))
 
         def new_a(q):
             a_t[q] = keep.tile([P, 1024], I32, name="a_t", tag="a_t%d" % q, align_bytes=64)
@@ -139,13 +141,13 @@ def tile_ternarylineartorch_kernel(tc, x, weight, bias, gamma, out):
             nat = nats[q][0]
             nc.vector.tensor_scalar(
                 out=a_t[q][:],
-                in0=nat[:].rearrange("p b k -> p (b k)").bitcast(I32),
+                in0=nat.rearrange("p b k -> p (b k)").bitcast(I32),
                 scalar1=ABS_MASK,
                 scalar2=None,
                 op0=ALU.bitwise_and,
             )
 
-        def w_sums(q):
+        def w_sums(q, end=False):
             cols = a_t[q][:].bitcast(BF16)
             for j in range(16):
                 nc.tensor.matmul(
@@ -153,7 +155,7 @@ def tile_ternarylineartorch_kernel(tc, x, weight, bias, gamma, out):
                     lhsT=cols[:, 128 * j : 128 * j + 128],
                     rhs=ones_bf[:, 0:NSUM],
                     start=(q == 0 and j == 0),
-                    stop=(q == NQ - 1 and j == 15),
+                    stop=(end and j == 15),
                 )
 
         xgs = {}
@@ -331,7 +333,14 @@ def tile_ternarylineartorch_kernel(tc, x, weight, bias, gamma, out):
 
         for d in range(ND - 1):
             load_w(d)
+            if d == ND - 2:
+                load_w_halves(ND - 1)
+                for ip in range(3):
+                    load_x(ip)
             for q in (2 * d, 2 * d + 1):
+                if q == 13:
+                    new_a(14)
+                    nat_abs(14)
                 if q >= 1:
                     new_a(q - 1)
                     w_abs(q - 1)
@@ -344,32 +353,54 @@ def tile_ternarylineartorch_kernel(tc, x, weight, bias, gamma, out):
                 if q == 3:
                     nc.tensor.transpose(th_ps[:, 0:128], brow_f[:], ident[:])
                     nc.vector.tensor_copy(out=bias_col[:], in_=th_ps[:, 0:16])
-        for gg in range(2):
-            load_w_half(ND - 1, gg)
-        for ip in range(4):
-            load_x(ip)
-        new_a(NQ - 3)
-        w_abs(NQ - 3)
-        w_sums(NQ - 5)
-        w_sums(NQ - 4)
-        new_a(NQ - 2)
-        nat_abs(NQ - 2)
-        w_sums(NQ - 3)
-        w_unit(NQ - 2)
-        w_sums(NQ - 2)
-        new_a(NQ - 1)
-        nat_abs(NQ - 1)
-        w_sums(NQ - 1)
+        load_x(3)
+        new_a(15)
+        nat_abs(15)
+        new_a(13)
+        w_abs(13)
+        w_sums(11)
+        w_sums(14)
+        w_sums(12)
+        w_sums(15)
+        w_sums(13, end=True)
         nc.vector.tensor_copy(out=ssum_sb[:], in_=ssum_ps[:, 0:NSUM])
         th2_ps = bank(1, "th2_ps")
         nc.tensor.matmul(out=th2_ps[:, 0:NSUM], lhsT=ones_f[:], rhs=ssum_sb[:], start=True, stop=True)
         nc.vector.tensor_scalar(out=t_sb[:], in0=th2_ps[:, 0:1], scalar1=0.5 / (N * K), scalar2=None, op0=ALU.mult)
         mask(0)
-        w_unit(NQ - 1)
         x_pair(0, (4, 5, 6, 7))
-        x_pair(1, (4, 5, 6, 7))
+        x_pair(1, (2, 3, 4, 5))
 
-        for q in range(NQ):
+        signed(0)
+        w_quant(0)
+        x_quant(0)
+        x_pair(2, (6, 7, 4, 5))
+        mask(1)
+        x_quant(1)
+        passes_s(0, 0)
+        x_pair(3, (6, 7, 2, 3))
+        signed(1)
+        w_quant(1)
+        passes_s(1, 0)
+        s_first(0, 0)
+        w_unit(14, (4, 5))
+        w_unit(15, (6, 7))
+        x_quant(2)
+        mask(2)
+        signed(2)
+        x_quant(3)
+        passes_s(0, 1)
+        passes_s(1, 1)
+        s_first(0, 1)
+        w_quant(2)
+        mask(3)
+        passes_s(2, 0)
+        passes_s(2, 1)
+        back(0, 0)
+        back(0, 1)
+        s_second(0, 0)
+        s_second(0, 1)
+        for q in range(3, NQ):
             d, gg = divmod(q, 2)
             signed(q)
             if q + 1 < NQ:
@@ -377,44 +408,9 @@ def tile_ternarylineartorch_kernel(tc, x, weight, bias, gamma, out):
                     w_abs(q + 1)
                 mask(q + 1)
             w_quant(q)
-            if q == 0:
-                x_quant(0)
-                x_quant(1)
-                x_pair(2, (2, 3, 6, 7))
-                passes_s(0, 0)
-                x_pair(3, (2, 3, 6, 7))
-                continue
-            if q == 1:
-                x_quant(2)
-                passes_s(1, 0)
-                s_first(0, 0)
-                continue
-            if q == 2:
-                passes_s(2, 0)
-                x_quant(3)
-                back(0, 0)
-                s_second(0, 0)
-                for qq in (0, 1):
-                    passes_s(qq, 1)
-                s_first(0, 1)
-                passes_s(2, 1)
-                continue
-            if q == 3:
-                passes_s(3, 0)
-                s_first(1, 0)
-                back(0, 1)
-                s_second(0, 1)
-                passes_s(3, 1)
-                s_first(1, 1)
-                continue
-            if gg == 0:
-                if d - 1 >= 0 and not transposed(d - 1, 0):
-                    add_v(d - 1, 0)
-                    gain_v(d - 1, 0)
-            else:
-                if d - 1 >= 0 and not transposed(d - 1, 1):
-                    add_v(d - 1, 1)
-                    gain_v(d - 1, 1)
+            if not transposed(d - 1, gg):
+                add_v(d - 1, gg)
+                gain_v(d - 1, gg)
             if d == ND - 1:
                 if gg == 0:
                     passes_last(0, range(6))
@@ -427,14 +423,14 @@ def tile_ternarylineartorch_kernel(tc, x, weight, bias, gamma, out):
                         passes_s(q, h)
                     elif gg == 1:
                         passes_v(d, h)
-            if d < ND - 1 and gg == 1:
                 for h in range(2):
-                    if transposed(d, h):
+                    if gg == 1 and transposed(d, h):
                         s_first(d, h)
-            if gg == 0:
                 for h in range(2):
-                    if transposed(d - 1, h):
+                    if gg == 0 and transposed(d - 1, h):
                         back(d - 1, h)
+                for h in range(2):
+                    if gg == 0 and transposed(d - 1, h):
                         s_second(d - 1, h)
         for h in range(2):
             last(h)

@@ -16,12 +16,15 @@ P = 128
 M, K, N = 1024, 2048, 2048
 FLOPS = 2 * M * K * N
 ABS_MASK = 0x7FFF7FFF
-SIGN_MASK = -0x7FFF8000
+TOP_MASK = -0x3FFF4000
+LOW16 = -65536
+TWO = 2.0 / (1.0 + 2.0**-8)
 NSUM = 32
 ND = N // 256
 NQ = 2 * ND
-S_FULL = 4
-S_HALF = 6
+S_PAIRS = (0, 1, 3, 5)
+M_FIRST = 99
+LEAD = 3
 
 
 def tile_ternarylineartorch_kernel(tc, x, weight, bias, gamma, out):
@@ -29,8 +32,10 @@ def tile_ternarylineartorch_kernel(tc, x, weight, bias, gamma, out):
     with ExitStack() as ctx:
         const = ctx.enter_context(tc.tile_pool(name="const", bufs=1))
         keep = ctx.enter_context(tc.tile_pool(name="keep", bufs=1))
+        absp = ctx.enter_context(tc.tile_pool(name="absp", bufs=2))
+        abs4 = ctx.enter_context(tc.tile_pool(name="abs4", bufs=4))
         xgp = ctx.enter_context(tc.tile_pool(name="xgp", bufs=2))
-        yp = ctx.enter_context(tc.tile_pool(name="yp", bufs=3))
+        yp = ctx.enter_context(tc.tile_pool(name="yp", bufs=2))
         psum = ctx.enter_context(tc.psum_pool(name="psum", bufs=1))
         ctx.enter_context(tc.manual_schedule())
 
@@ -56,6 +61,9 @@ def tile_ternarylineartorch_kernel(tc, x, weight, bias, gamma, out):
         bias_col = const.tile([P, 16], F32, name="bias_col")
         ssum_sb = const.tile([P, NSUM], F32, name="ssum_sb")
         t_sb = const.tile([P, 1], F32, name="t_sb")
+        t_low = const.tile([P, 1], I32, name="t_low")
+        t_inv = const.tile([P, 1], F32, name="t_inv")
+        s_sb = const.tile([P, 1], F32, name="s_sb")
         bias_bc = const.tile([P, N], BF16, name="bias_bc")
 
         for c in range(4):
@@ -66,8 +74,8 @@ def tile_ternarylineartorch_kernel(tc, x, weight, bias, gamma, out):
             nc.scalar.copy(out=bias_bc[:, 512 * c : 512 * c + 512], in_=bb[:])
 
         w_t = [None] * NQ
-        a_t = [None] * NQ
         w_sc = [keep.tile([P, 512], U8, name="w_sc%d" % q, align_bytes=64) for q in range(NQ)]
+        w_codes = [keep.tile([P, 512], U32, name="w_codes%d" % q, align_bytes=64) for q in range(NQ)]
         x_codes = [keep.tile([P, 4, 512], U32, name="x_codes%d" % h, align_bytes=64) for h in range(2)]
         x_sc = [keep.tile([P, 4, 512], U8, name="x_sc%d" % h, align_bytes=64) for h in range(2)]
 
@@ -77,23 +85,28 @@ def tile_ternarylineartorch_kernel(tc, x, weight, bias, gamma, out):
         slot = [0]
 
         def stage(shape, name):
-            t = keep.tile(shape, BF16, name=name, tag="nat%d" % (slot[0] % 5), align_bytes=64)
+            t = keep.tile(shape, BF16, name=name, tag="nat%d" % (slot[0] % 7), align_bytes=64)
             slot[0] += 1
             return t
 
         nats = {}
+        whole = {}
 
         def load_w(d):
             nat = stage([P, 2, K], "wn")
             nc.sync.dma_start(out=nat[:], in_=weight[256 * d : 256 * d + 256, :].rearrange("(b p) k -> p b k", p=P))
+            whole[d] = nat
             for gg in range(2):
                 nats[2 * d + gg] = (nat, 512 * gg)
 
         def load_w_halves(d):
             nat = stage([P, 2, 2, K // 2], "wh")
             for gg in range(2):
-                src = weight[256 * d : 256 * d + 256, 1024 * gg : 1024 * gg + 1024]
-                nc.sync.dma_start(out=nat[:, gg, :, :], in_=src.rearrange("(b p) k -> p b k", p=P))
+                for b in range(2):
+                    r0 = 256 * d + 128 * b
+                    nc.sync.dma_start(
+                        out=nat[:, gg, b, :], in_=weight[r0 : r0 + 128, 1024 * gg : 1024 * gg + 1024]
+                    )
                 nats[2 * d + gg] = (nat[:, gg, :, :], 0)
 
         xnats = {}
@@ -115,11 +128,12 @@ def tile_ternarylineartorch_kernel(tc, x, weight, bias, gamma, out):
             else:
                 nc.scalar.copy(out=dst, in_=src)
 
-        def w_unit(q, banks=None):
+        def w_unit(q, banks, vector_banks, parts=(0, 1)):
             nat, base = nats[q]
-            w_t[q] = keep.tile([P, 1024], I32, name="w_t", tag="w_t%d" % q, align_bytes=64)
-            for gi in range(2):
-                tp = bank(banks[gi] if banks else 2 + (2 * q + gi) % 6, "wtp")
+            if 0 in parts:
+                w_t[q] = keep.tile([P, 2048], BF16, name="w_t", tag="w_t%d" % q, align_bytes=64)
+            for gi in parts:
+                tp = bank(banks[gi], "wtp")
                 srcs = []
                 for b in range(2):
                     words = nat[:, b, :].bitcast(F32)
@@ -127,35 +141,26 @@ def tile_ternarylineartorch_kernel(tc, x, weight, bias, gamma, out):
                         col = base + 256 * gi + 128 * u
                         srcs.append(words[:, col : col + 128])
                 four_transposes(tp, srcs)
-                copy_out(gi == 1 and q % 2 == 1 and q < 12, tp, w_t[q][:, 512 * gi : 512 * gi + 512].bitcast(F32))
+                copy_out(gi in vector_banks, tp, w_t[q][:].bitcast(F32)[:, 512 * gi : 512 * gi + 512])
 
-        def new_a(q):
-            a_t[q] = keep.tile([P, 1024], I32, name="a_t", tag="a_t%d" % q, align_bytes=64)
+        mags = {}
 
-        def w_abs(q):
-            nc.vector.tensor_scalar(
-                out=a_t[q][:], in0=w_t[q][:], scalar1=ABS_MASK, scalar2=None, op0=ALU.bitwise_and
-            )
+        def w_abs(key, words):
+            n = words.shape[-1]
+            mag = (absp if n > 512 else abs4).tile([P, n], I32, name="mag", tag="mag%d" % n, align_bytes=64)
+            nc.vector.tensor_scalar(out=mag[:], in0=words, scalar1=ABS_MASK, scalar2=None, op0=ALU.bitwise_and)
+            mags[key] = mag
 
-        def nat_abs(q):
-            nat = nats[q][0]
-            nc.vector.tensor_scalar(
-                out=a_t[q][:],
-                in0=nat.rearrange("p b k -> p (b k)").bitcast(I32),
-                scalar1=ABS_MASK,
-                scalar2=None,
-                op0=ALU.bitwise_and,
-            )
-
-        def w_sums(q, end=False):
-            cols = a_t[q][:].bitcast(BF16)
-            for j in range(16):
+        def w_sums(key, first=False, end=False):
+            cols = mags[key][:].bitcast(BF16)
+            blocks = cols.shape[-1] // P
+            for j in range(blocks):
                 nc.tensor.matmul(
                     out=ssum_ps[:, 0:NSUM],
                     lhsT=cols[:, 128 * j : 128 * j + 128],
                     rhs=ones_bf[:, 0:NSUM],
-                    start=(q == 0 and j == 0),
-                    stop=(end and j == 15),
+                    start=(first and j == 0),
+                    stop=(end and j == blocks - 1),
                 )
 
         xgs = {}
@@ -183,29 +188,29 @@ def tile_ternarylineartorch_kernel(tc, x, weight, bias, gamma, out):
                     in_=xgs[ip][:, g, :].bitcast(BF16),
                 )
 
-        def mask(q):
-            a_bf = a_t[q][:].bitcast(BF16)
-            nc.vector.tensor_scalar(out=a_bf, in0=a_bf, scalar1=t_sb[:, 0:1], scalar2=None, op0=ALU.is_gt)
+        def on_scalar(q):
+            return q % 2 == 1 and q >= M_FIRST
 
-        def signed(q):
-            nc.vector.scalar_tensor_tensor(
-                out=a_t[q][:],
-                in0=w_t[q][:],
-                scalar=SIGN_MASK,
-                in1=a_t[q][:],
-                op0=ALU.bitwise_and,
-                op1=ALU.bitwise_or,
-            )
+        def scale_up(q):
+            if on_scalar(q):
+                nc.scalar.activation(out=w_t[q][:], in_=w_t[q][:], func=ACT.Copy, scale=s_sb[:, 0:1])
+            else:
+                nc.vector.tensor_scalar(
+                    out=w_t[q][:], in0=w_t[q][:], scalar1=t_inv[:, 0:1], scalar2=TWO, op0=ALU.mult, op1=ALU.mult
+                )
 
-        w_codes = {}
+        def cut(q):
+            words = w_t[q][:].bitcast(I32)
+            nc.vector.tensor_scalar(out=words, in0=words, scalar1=TOP_MASK, scalar2=None, op0=ALU.bitwise_and)
+
+        def halve(q):
+            nc.vector.tensor_scalar(out=w_t[q][:], in0=w_t[q][:], scalar1=0.5, scalar2=None, op0=ALU.mult)
 
         def w_quant(q):
-            codes = keep.tile([P, 512], U32, name="w_codes", tag="w_t%d" % q, align_bytes=64)
-            nc.vector.quantize_mx(out=codes[:].bitcast(FP8X4), scales=w_sc[q][:], in_=a_t[q][:].bitcast(BF16))
-            w_codes[q] = codes
+            nc.vector.quantize_mx(out=w_codes[q][:].bitcast(FP8X4), scales=w_sc[q][:], in_=w_t[q][:])
 
         def transposed(d, h):
-            return d < S_FULL or (d < S_HALF and h == 0)
+            return d in S_PAIRS
 
         accs = {}
 
@@ -259,7 +264,7 @@ def tile_ternarylineartorch_kernel(tc, x, weight, bias, gamma, out):
             return out[r0 : r0 + nrows, 256 * d : 256 * d + 256].rearrange("(t p) n -> p t n", p=P)
 
         def new_o(d, h):
-            return keep.tile([P, 2, 512], F32, name="o", tag="a_t%d" % (2 * d + h), align_bytes=64)
+            return keep.tile([P, 2, 512], F32, name="o", tag="w_t%d" % (2 * d + h), align_bytes=64)
 
         ovs = {}
 
@@ -333,67 +338,69 @@ def tile_ternarylineartorch_kernel(tc, x, weight, bias, gamma, out):
 
         for d in range(ND - 1):
             load_w(d)
+        for d in range(ND - 1):
+            w_abs(d, whole[d][:].rearrange("p b k -> p (b k)").bitcast(I32))
+            if d == 0:
+                nc.vector.tensor_copy(out=gam_f[:], in_=gam_bf[:])
+                nc.vector.tensor_copy(out=brow_f[:], in_=brow_bf[:])
             if d == ND - 2:
-                load_w_halves(ND - 1)
-                for ip in range(3):
-                    load_x(ip)
+                for key in range(4):
+                    w_abs("h%d" % key, nats[NQ - 2 + key // 2][0][:, key % 2, :].bitcast(I32))
             for q in (2 * d, 2 * d + 1):
-                if q == 13:
-                    new_a(14)
-                    nat_abs(14)
-                if q >= 1:
-                    new_a(q - 1)
-                    w_abs(q - 1)
-                w_unit(q)
-                if q >= 3:
-                    w_sums(q - 3)
-                if q == 1:
-                    nc.vector.tensor_copy(out=gam_f[:], in_=gam_bf[:])
-                    nc.vector.tensor_copy(out=brow_f[:], in_=brow_bf[:])
-                if q == 3:
-                    nc.tensor.transpose(th_ps[:, 0:128], brow_f[:], ident[:])
-                    nc.vector.tensor_copy(out=bias_col[:], in_=th_ps[:, 0:16])
-        load_x(3)
-        new_a(15)
-        nat_abs(15)
-        new_a(13)
-        w_abs(13)
-        w_sums(11)
-        w_sums(14)
-        w_sums(12)
-        w_sums(15)
-        w_sums(13, end=True)
+                w_unit(q, [2 + (2 * q + gi) % 6 for gi in range(2)], (1,) if q % 2 == 1 and d < ND - 2 else ())
+            w_sums(d, first=(d == 0))
+            if d == 0:
+                load_w_halves(ND - 1)
+            if 1 <= d <= 4:
+                load_x(d - 1)
+            if d == 1:
+                nc.tensor.transpose(th_ps[:, 0:128], brow_f[:], ident[:])
+                nc.vector.tensor_copy(out=bias_col[:], in_=th_ps[:, 0:16])
+        for key in range(4):
+            w_sums("h%d" % key, end=(key == 3))
+        w_unit(NQ - 2, (2, 3), (), (0,))
         nc.vector.tensor_copy(out=ssum_sb[:], in_=ssum_ps[:, 0:NSUM])
         th2_ps = bank(1, "th2_ps")
         nc.tensor.matmul(out=th2_ps[:, 0:NSUM], lhsT=ones_f[:], rhs=ssum_sb[:], start=True, stop=True)
-        nc.vector.tensor_scalar(out=t_sb[:], in0=th2_ps[:, 0:1], scalar1=0.5 / (N * K), scalar2=None, op0=ALU.mult)
-        mask(0)
-        x_pair(0, (4, 5, 6, 7))
-        x_pair(1, (2, 3, 4, 5))
+        w_unit(NQ - 2, (2, 3), (), (1,))
+        w_unit(NQ - 1, (4, 5), ())
+        nc.vector.tensor_scalar(
+            out=t_sb[:], in0=th2_ps[:, 0:1], scalar1=0.5 / (N * K), scalar2=2.0**-100, op0=ALU.mult, op1=ALU.max
+        )
+        nc.vector.tensor_scalar(
+            out=t_low[:], in0=t_sb[:].bitcast(I32), scalar1=LOW16, scalar2=None, op0=ALU.bitwise_and
+        )
+        nc.vector.reciprocal(out=t_inv[:], in_=t_low[:].bitcast(F32))
+        x_pair(0, (6, 7, 2, 3))
+        x_pair(1, (4, 5, 6, 7))
 
-        signed(0)
+        scale_up(0)
+        nc.vector.tensor_scalar(out=s_sb[:], in0=t_inv[:], scalar1=TWO, scalar2=None, op0=ALU.mult)
+        cut(0)
+        scale_up(1)
+        halve(0)
+        cut(1)
         w_quant(0)
         x_quant(0)
-        x_pair(2, (6, 7, 4, 5))
-        mask(1)
+        x_pair(2, (2, 3, 4, 5))
+        halve(1)
         x_quant(1)
         passes_s(0, 0)
         x_pair(3, (6, 7, 2, 3))
-        signed(1)
+        scale_up(2)
         w_quant(1)
         passes_s(1, 0)
         s_first(0, 0)
-        w_unit(14, (4, 5))
-        w_unit(15, (6, 7))
         x_quant(2)
-        mask(2)
-        signed(2)
+        cut(2)
         x_quant(3)
+        halve(2)
         passes_s(0, 1)
         passes_s(1, 1)
         s_first(0, 1)
+        scale_up(3)
         w_quant(2)
-        mask(3)
+        cut(3)
         passes_s(2, 0)
         passes_s(2, 1)
         back(0, 0)
@@ -402,12 +409,14 @@ def tile_ternarylineartorch_kernel(tc, x, weight, bias, gamma, out):
         s_second(0, 1)
         for q in range(3, NQ):
             d, gg = divmod(q, 2)
-            signed(q)
+            if q + 1 < NQ and not on_scalar(q + 1):
+                scale_up(q + 1)
+            halve(q)
             if q + 1 < NQ:
-                if q + 1 >= NQ - 2:
-                    w_abs(q + 1)
-                mask(q + 1)
+                cut(q + 1)
             w_quant(q)
+            if q + LEAD < NQ and on_scalar(q + LEAD):
+                scale_up(q + LEAD)
             if not transposed(d - 1, gg):
                 add_v(d - 1, gg)
                 gain_v(d - 1, gg)

@@ -22,8 +22,8 @@ TWO = 2.0 / (1.0 + 2.0**-8)
 NSUM = 32
 ND = N // 256
 NQ = 2 * ND
-S_PAIRS = (0, 1, 3, 5)
-M_FIRST = 99
+S_PAIRS = (0, 1, 3)
+M_FIRST = 7
 LEAD = 3
 
 
@@ -189,7 +189,7 @@ def tile_ternarylineartorch_kernel(tc, x, weight, bias, gamma, out):
                 )
 
         def on_scalar(q):
-            return q % 2 == 1 and q >= M_FIRST
+            return q - LEAD >= M_FIRST and (q - LEAD) // 2 - 1 not in S_PAIRS
 
         def scale_up(q):
             if on_scalar(q):
@@ -415,9 +415,9 @@ def tile_ternarylineartorch_kernel(tc, x, weight, bias, gamma, out):
             if q + 1 < NQ:
                 cut(q + 1)
             w_quant(q)
-            if q + LEAD < NQ and on_scalar(q + LEAD):
-                scale_up(q + LEAD)
             if not transposed(d - 1, gg):
+                if q + LEAD < NQ and on_scalar(q + LEAD):
+                    scale_up(q + LEAD)
                 add_v(d - 1, gg)
                 gain_v(d - 1, gg)
             if d == ND - 1:

@@ -22,9 +22,9 @@ TWO = 2.0 / (1.0 + 2.0**-8)
 NSUM = 32
 ND = N // 256
 NQ = 2 * ND
-S_PAIRS = (0, 1, 3)
-M_FIRST = 7
-LEAD = 3
+S_PAIRS = (0, 1, 3, 5)
+M_FIRST = 6
+LEAD = 4
 
 
 def tile_ternarylineartorch_kernel(tc, x, weight, bias, gamma, out):
@@ -112,8 +112,10 @@ def tile_ternarylineartorch_kernel(tc, x, weight, bias, gamma, out):
         xnats = {}
 
         def load_x(ip):
-            nat = stage([P, 2, K], "xn")
-            nc.sync.dma_start(out=nat[:], in_=x[256 * ip : 256 * ip + 256, :].rearrange("(b p) k -> p b k", p=P))
+            nat = stage([P, 2, 2, K // 2], "xn")
+            for e in range(2):
+                src = x[256 * ip : 256 * ip + 256, 1024 * e : 1024 * e + 1024]
+                nc.sync.dma_start(out=nat[:, e, :, :], in_=src.rearrange("(b p) k -> p b k", p=P))
             xnats[ip] = nat
 
         def four_transposes(tp, sources):
@@ -171,9 +173,9 @@ def tile_ternarylineartorch_kernel(tc, x, weight, bias, gamma, out):
                 tp = bank(banks[g], "xtp")
                 srcs = []
                 for b in range(2):
-                    words = xnats[ip][:, b, :].bitcast(F32)
+                    words = xnats[ip][:, g // 2, b, :].bitcast(F32)
                     for u in range(2):
-                        col = 256 * g + 128 * u
+                        col = 256 * (g % 2) + 128 * u
                         srcs.append(words[:, col : col + 128])
                 four_transposes(tp, srcs)
                 copy_out(False, tp, xg[:, g, :])
@@ -299,10 +301,10 @@ def tile_ternarylineartorch_kernel(tc, x, weight, bias, gamma, out):
                         in1=bias_bc[:, 256 * d : 256 * d + 256],
                         op=ALU.add,
                     )
-                nc.scalar.activation(out=o[:, b, :], in_=o[:, b, :], func=ACT.Copy, scale=gam_f[:, 0:1])
-                nc.sync.dma_start(
-                    out=rows(512 * h + 256 * b, 256, d), in_=o[:, b, :].rearrange("p (t n) -> p t n", t=2)
-                )
+                    piece = o[:, b, 256 * t : 256 * t + 256]
+                    nc.scalar.activation(out=piece, in_=piece, func=ACT.Copy, scale=gam_f[:, 0:1])
+                    r0 = 512 * h + 256 * b + 128 * t
+                    nc.sync.dma_start(out=out[r0 : r0 + 128, 256 * d : 256 * d + 256], in_=piece)
 
         ys = {}
 

@@ -19,7 +19,7 @@ ABS_MASK = 0x7FFF7FFF
 TOP_MASK = -0x3FFF4000
 LOW16 = -65536
 TWO = 2.0 / (1.0 + 2.0**-8)
-NSUM = 32
+NSUM = 48
 ND = N // 256
 NQ = 2 * ND
 S_PAIRS = (0, 1, 3, 5)
@@ -80,7 +80,6 @@ def tile_ternarylineartorch_kernel(tc, x, weight, bias, gamma, out):
         x_sc = [keep.tile([P, 4, 512], U8, name="x_sc%d" % h, align_bytes=64) for h in range(2)]
 
         ssum_ps = bank(0, "ssum_ps")
-        th_ps = bank(1, "th_ps")
 
         slot = [0]
 
@@ -153,10 +152,16 @@ def tile_ternarylineartorch_kernel(tc, x, weight, bias, gamma, out):
             nc.vector.tensor_scalar(out=mag[:], in0=words, scalar1=ABS_MASK, scalar2=None, op0=ALU.bitwise_and)
             mags[key] = mag
 
-        def w_sums(key, first=False, end=False):
+        def keep_clock(n, k, rhs):
+            for i in range(n):
+                dummy = bank(k, "dummy")
+                nc.tensor.matmul(out=dummy[:], lhsT=ones_bf[:], rhs=rhs[:, 0:512], start=True, stop=True)
+
+        def w_sums(key, first=False, end=False, half=None):
             cols = mags[key][:].bitcast(BF16)
             blocks = cols.shape[-1] // P
-            for j in range(blocks):
+            lo, hi = (0, blocks) if half is None else (half * blocks // 2, (half + 1) * blocks // 2)
+            for j in range(lo, hi):
                 nc.tensor.matmul(
                     out=ssum_ps[:, 0:NSUM],
                     lhsT=cols[:, 128 * j : 128 * j + 128],
@@ -350,14 +355,21 @@ def tile_ternarylineartorch_kernel(tc, x, weight, bias, gamma, out):
                     w_abs("h%d" % key, nats[NQ - 2 + key // 2][0][:, key % 2, :].bitcast(I32))
             for q in (2 * d, 2 * d + 1):
                 w_unit(q, [2 + (2 * q + gi) % 6 for gi in range(2)], (1,) if q % 2 == 1 and d < ND - 2 else ())
-            w_sums(d, first=(d == 0))
+                if d == 0:
+                    keep_clock(2, 1, brow1)
+                if q % 2 == 1:
+                    w_sums(d, first=(d == 0), half=0)
+                elif d >= 1:
+                    w_sums(d - 1, half=1)
             if d == 0:
                 load_w_halves(ND - 1)
             if 1 <= d <= 4:
                 load_x(d - 1)
             if d == 1:
-                nc.tensor.transpose(th_ps[:, 0:128], brow_f[:], ident[:])
-                nc.vector.tensor_copy(out=bias_col[:], in_=th_ps[:, 0:16])
+                bc = bank(1, "bc")
+                nc.tensor.transpose(bc[:, 0:128], brow_f[:], ident[:])
+                nc.vector.tensor_copy(out=bias_col[:], in_=bc[:, 0:16])
+        w_sums(ND - 2, half=1)
         for key in range(4):
             w_sums("h%d" % key, end=(key == 3))
         w_unit(NQ - 2, (2, 3), (), (0,))
@@ -374,7 +386,9 @@ def tile_ternarylineartorch_kernel(tc, x, weight, bias, gamma, out):
         )
         nc.vector.reciprocal(out=t_inv[:], in_=t_low[:].bitcast(F32))
         x_pair(0, (6, 7, 2, 3))
+        keep_clock(2, 0, bias_bc)
         x_pair(1, (4, 5, 6, 7))
+        keep_clock(2, 0, bias_bc)
 
         scale_up(0)
         nc.vector.tensor_scalar(out=s_sb[:], in0=t_inv[:], scalar1=TWO, scalar2=None, op0=ALU.mult)
@@ -385,6 +399,7 @@ def tile_ternarylineartorch_kernel(tc, x, weight, bias, gamma, out):
         w_quant(0)
         x_quant(0)
         x_pair(2, (2, 3, 4, 5))
+        keep_clock(1, 0, bias_bc)
         halve(1)
         x_quant(1)
         passes_s(0, 0)

@@ -22,9 +22,9 @@ TWO = 2.0 / (1.0 + 2.0**-8)
 NSUM = 48
 ND = N // 256
 NQ = 2 * ND
-S_PAIRS = (0, 1, 3, 5)
+S_PAIRS = (0, 1, 3)
 M_FIRST = 6
-LEAD = 4
+LEAD = 3
 
 
 def tile_ternarylineartorch_kernel(tc, x, weight, bias, gamma, out):
@@ -42,6 +42,8 @@ def tile_ternarylineartorch_kernel(tc, x, weight, bias, gamma, out):
         def bank(k, name):
             return psum.tile([P, 512], F32, tag="b%d" % k, name=name)
 
+        ones_bf = const.tile([P, P], BF16, name="ones_bf")
+        nc.vector.memset(ones_bf[:], 1.0)
         gam_bf = const.tile([P, 1], BF16, name="gam_bf")
         nc.sync.dma_start(out=gam_bf[:], in_=gamma.partition_broadcast(P))
         brow_bf = const.tile([P, P], BF16, name="brow_bf")
@@ -52,8 +54,6 @@ def tile_ternarylineartorch_kernel(tc, x, weight, bias, gamma, out):
         nc.sync.dma_start(out=brow1[0:1, :], in_=bias.unsqueeze(0))
         ident = const.tile([P, P], F32, name="ident")
         make_identity(nc, ident[:])
-        ones_bf = const.tile([P, P], BF16, name="ones_bf")
-        nc.vector.memset(ones_bf[:], 1.0)
         ones_f = const.tile([P, P], F32, name="ones_f")
         nc.vector.memset(ones_f[:], 1.0)
         gam_f = const.tile([P, 1], F32, name="gam_f")
@@ -66,8 +66,18 @@ def tile_ternarylineartorch_kernel(tc, x, weight, bias, gamma, out):
         s_sb = const.tile([P, 1], F32, name="s_sb")
         bias_bc = const.tile([P, N], BF16, name="bias_bc")
 
+        ones_wide = keep.tile([P, 512], BF16, name="ones_wide", tag="w_t14", align_bytes=64)
+        nc.vector.memset(ones_wide[:], 1.0)
+
+        def keep_clock(n, k, rhs):
+            for i in range(n):
+                dummy = bank(k, "dummy")
+                nc.tensor.matmul(out=dummy[:], lhsT=ones_bf[:], rhs=rhs[:, 0:512], start=True, stop=True)
+
+        keep_clock(2, 1, ones_wide)
+
         for c in range(4):
-            bb = bank(2 + c, "bb")
+            bb = bank((6, 7, 5, 4)[c], "bb")
             nc.tensor.matmul(
                 out=bb[:], lhsT=ones_bf[:], rhs=brow1[:, 512 * c : 512 * c + 512], start=True, stop=True
             )
@@ -97,6 +107,13 @@ def tile_ternarylineartorch_kernel(tc, x, weight, bias, gamma, out):
             whole[d] = nat
             for gg in range(2):
                 nats[2 * d + gg] = (nat, 512 * gg)
+
+        def load_w_first(d):
+            nat = stage([P, 2, 2, K // 2], "wf")
+            for gg in range(2):
+                src = weight[256 * d : 256 * d + 256, 1024 * gg : 1024 * gg + 1024]
+                nc.sync.dma_start(out=nat[:, gg, :, :], in_=src.rearrange("(b p) k -> p b k", p=P))
+                nats[2 * d + gg] = (nat[:, gg, :, :], 0)
 
         def load_w_halves(d):
             nat = stage([P, 2, 2, K // 2], "wh")
@@ -145,23 +162,18 @@ def tile_ternarylineartorch_kernel(tc, x, weight, bias, gamma, out):
                 copy_out(gi in vector_banks, tp, w_t[q][:].bitcast(F32)[:, 512 * gi : 512 * gi + 512])
 
         mags = {}
+        bcs = []
 
         def w_abs(key, words):
             n = words.shape[-1]
-            mag = (absp if n > 512 else abs4).tile([P, n], I32, name="mag", tag="mag%d" % n, align_bytes=64)
+            mag = (absp if n > 512 else abs4).tile([P, n], I32, name="mag", tag="mag" if n > 512 else "magq", align_bytes=64)
             nc.vector.tensor_scalar(out=mag[:], in0=words, scalar1=ABS_MASK, scalar2=None, op0=ALU.bitwise_and)
             mags[key] = mag
 
-        def keep_clock(n, k, rhs):
-            for i in range(n):
-                dummy = bank(k, "dummy")
-                nc.tensor.matmul(out=dummy[:], lhsT=ones_bf[:], rhs=rhs[:, 0:512], start=True, stop=True)
-
-        def w_sums(key, first=False, end=False, half=None):
+        def w_sums(key, first=False, end=False):
             cols = mags[key][:].bitcast(BF16)
             blocks = cols.shape[-1] // P
-            lo, hi = (0, blocks) if half is None else (half * blocks // 2, (half + 1) * blocks // 2)
-            for j in range(lo, hi):
+            for j in range(blocks):
                 nc.tensor.matmul(
                     out=ssum_ps[:, 0:NSUM],
                     lhsT=cols[:, 128 * j : 128 * j + 128],
@@ -251,13 +263,21 @@ def tile_ternarylineartorch_kernel(tc, x, weight, bias, gamma, out):
                 stop=(g == 3),
             )
 
+        def passes_v_early(d):
+            for h in range(2):
+                for b in range(2):
+                    acc = bank(4 * (d % 2) + 2 * h + b, "acc_v")
+                    for g in range(2):
+                        pass_v(acc[:, 0:256], d, h, 2 * b, g)
+                    accs[(d, h, b)] = acc
+
         def passes_v(d, h):
             for b in range(2):
-                acc = bank(4 * (d % 2) + 2 * h + b, "acc_v")
-                for t in range(2):
-                    for g in range(4):
-                        pass_v(acc[:, 256 * t : 256 * t + 256], d, h, 2 * b + t, g)
-                accs[(d, h, b)] = acc
+                acc = accs[(d, h, b)]
+                for g in range(2, 4):
+                    pass_v(acc[:, 0:256], d, h, 2 * b, g)
+                for g in range(4):
+                    pass_v(acc[:, 256:512], d, h, 2 * b + 1, g)
 
         def passes_last(gg, tiles):
             d = ND - 1
@@ -343,10 +363,17 @@ def tile_ternarylineartorch_kernel(tc, x, weight, bias, gamma, out):
                     out=rows(512 * h + 256 * b, 256, d), in_=o[:, b, :].rearrange("p (t n) -> p t n", t=2)
                 )
 
-        for d in range(ND - 1):
+        load_w_first(0)
+        for d in range(1, ND - 1):
             load_w(d)
         for d in range(ND - 1):
-            w_abs(d, whole[d][:].rearrange("p b k -> p (b k)").bitcast(I32))
+            if d == 0:
+                for gg in range(2):
+                    w_abs("f%d" % gg, nats[gg][0].rearrange("p b k -> p (b k)").bitcast(I32))
+            else:
+                w_abs(d, whole[d][:].rearrange("p b k -> p (b k)").bitcast(I32))
+            if d == 2:
+                nc.vector.tensor_copy(out=bias_col[:], in_=bcs[0][:, 0:16])
             if d == 0:
                 nc.vector.tensor_copy(out=gam_f[:], in_=gam_bf[:])
                 nc.vector.tensor_copy(out=brow_f[:], in_=brow_bf[:])
@@ -356,11 +383,9 @@ def tile_ternarylineartorch_kernel(tc, x, weight, bias, gamma, out):
             for q in (2 * d, 2 * d + 1):
                 w_unit(q, [2 + (2 * q + gi) % 6 for gi in range(2)], (1,) if q % 2 == 1 and d < ND - 2 else ())
                 if d == 0:
-                    keep_clock(2, 1, brow1)
-                if q % 2 == 1:
-                    w_sums(d, first=(d == 0), half=0)
-                elif d >= 1:
-                    w_sums(d - 1, half=1)
+                    w_sums("f%d" % q, first=(q == 0))
+            if d > 0:
+                w_sums(d)
             if d == 0:
                 load_w_halves(ND - 1)
             if 1 <= d <= 4:
@@ -368,8 +393,7 @@ def tile_ternarylineartorch_kernel(tc, x, weight, bias, gamma, out):
             if d == 1:
                 bc = bank(1, "bc")
                 nc.tensor.transpose(bc[:, 0:128], brow_f[:], ident[:])
-                nc.vector.tensor_copy(out=bias_col[:], in_=bc[:, 0:16])
-        w_sums(ND - 2, half=1)
+                bcs.append(bc)
         for key in range(4):
             w_sums("h%d" % key, end=(key == 3))
         w_unit(NQ - 2, (2, 3), (), (0,))
@@ -435,8 +459,13 @@ def tile_ternarylineartorch_kernel(tc, x, weight, bias, gamma, out):
             if not transposed(d - 1, gg):
                 if q + LEAD < NQ and on_scalar(q + LEAD):
                     scale_up(q + LEAD)
-                add_v(d - 1, gg)
-                gain_v(d - 1, gg)
+                if d == ND - 1:
+                    add_v(d - 1, gg)
+                    gain_v(d - 1, gg)
+                elif gg == 1:
+                    for h in range(2):
+                        add_v(d - 1, h)
+                        gain_v(d - 1, h)
             if d == ND - 1:
                 if gg == 0:
                     passes_last(0, range(6))
@@ -444,6 +473,8 @@ def tile_ternarylineartorch_kernel(tc, x, weight, bias, gamma, out):
                     passes_last(0, range(6, 8))
                     passes_last(1, range(8))
             else:
+                if gg == 0 and not transposed(d, 0):
+                    passes_v_early(d)
                 for h in range(2):
                     if transposed(d, h):
                         passes_s(q, h)

@@ -25,6 +25,7 @@ NQ = 2 * ND
 S_PAIRS = (0, 1, 3)
 M_FIRST = 6
 LEAD = 3
+EARLY = 5
 
 
 def tile_ternarylineartorch_kernel(tc, x, weight, bias, gamma, out):
@@ -34,7 +35,7 @@ def tile_ternarylineartorch_kernel(tc, x, weight, bias, gamma, out):
         keep = ctx.enter_context(tc.tile_pool(name="keep", bufs=1))
         absp = ctx.enter_context(tc.tile_pool(name="absp", bufs=2))
         abs4 = ctx.enter_context(tc.tile_pool(name="abs4", bufs=4))
-        xgp = ctx.enter_context(tc.tile_pool(name="xgp", bufs=2))
+        xgp = ctx.enter_context(tc.tile_pool(name="xgp", bufs=1))
         yp = ctx.enter_context(tc.tile_pool(name="yp", bufs=2))
         psum = ctx.enter_context(tc.psum_pool(name="psum", bufs=1))
         ctx.enter_context(tc.manual_schedule())
@@ -182,10 +183,9 @@ def tile_ternarylineartorch_kernel(tc, x, weight, bias, gamma, out):
                     stop=(end and j == blocks - 1),
                 )
 
-        xgs = {}
+        xg = xgp.tile([P, 4, 2, 512], F32, name="xg", align_bytes=64)
 
         def x_pair(ip, banks):
-            xg = xgp.tile([P, 4, 512], F32, name="xg", align_bytes=64)
             for g in range(4):
                 tp = bank(banks[g], "xtp")
                 srcs = []
@@ -195,20 +195,18 @@ def tile_ternarylineartorch_kernel(tc, x, weight, bias, gamma, out):
                         col = 256 * (g % 2) + 128 * u
                         srcs.append(words[:, col : col + 128])
                 four_transposes(tp, srcs)
-                copy_out(False, tp, xg[:, g, :])
-            xgs[ip] = xg
+                copy_out(False, tp, xg[:, g, ip % 2, :])
 
-        def x_quant(ip):
-            h, t = divmod(ip, 2)
+        def x_quant(h):
             for g in range(4):
                 nc.vector.quantize_mx(
-                    out=x_codes[h][:, g, 256 * t : 256 * t + 256].bitcast(FP8X4),
-                    scales=x_sc[h][:, g, 256 * t : 256 * t + 256],
-                    in_=xgs[ip][:, g, :].bitcast(BF16),
+                    out=x_codes[h][:, g, :].bitcast(FP8X4),
+                    scales=x_sc[h][:, g, :],
+                    in_=xg[:, g, :, :].rearrange("p t w -> p (t w)").bitcast(BF16),
                 )
 
         def on_scalar(q):
-            return q - LEAD >= M_FIRST and (q - LEAD) // 2 - 1 not in S_PAIRS
+            return q == EARLY or (q - LEAD >= M_FIRST and (q - LEAD) // 2 - 1 not in S_PAIRS)
 
         def scale_up(q):
             if on_scalar(q):
@@ -421,28 +419,27 @@ def tile_ternarylineartorch_kernel(tc, x, weight, bias, gamma, out):
         halve(0)
         cut(1)
         w_quant(0)
+        halve(1)
+        scale_up(2)
+        w_quant(1)
         x_quant(0)
         x_pair(2, (2, 3, 4, 5))
         keep_clock(1, 0, bias_bc)
-        halve(1)
-        x_quant(1)
         passes_s(0, 0)
         x_pair(3, (6, 7, 2, 3))
-        scale_up(2)
-        w_quant(1)
         passes_s(1, 0)
         s_first(0, 0)
-        x_quant(2)
+        scale_up(EARLY)
         cut(2)
-        x_quant(3)
+        scale_up(3)
         halve(2)
+        cut(3)
+        w_quant(2)
+        passes_s(2, 0)
+        x_quant(1)
         passes_s(0, 1)
         passes_s(1, 1)
         s_first(0, 1)
-        scale_up(3)
-        w_quant(2)
-        cut(3)
-        passes_s(2, 0)
         passes_s(2, 1)
         back(0, 0)
         back(0, 1)
@@ -453,16 +450,20 @@ def tile_ternarylineartorch_kernel(tc, x, weight, bias, gamma, out):
             if q + 1 < NQ and not on_scalar(q + 1):
                 scale_up(q + 1)
             halve(q)
+            if q == NQ - 1:
+                add_v(d - 1, 1)
+                gain_v(d - 1, 1)
+                passes_last(0, range(6, 8))
             if q + 1 < NQ:
                 cut(q + 1)
             w_quant(q)
             if not transposed(d - 1, gg):
                 if q + LEAD < NQ and on_scalar(q + LEAD):
                     scale_up(q + LEAD)
-                if d == ND - 1:
-                    add_v(d - 1, gg)
-                    gain_v(d - 1, gg)
-                elif gg == 1:
+                if q == NQ - 2:
+                    add_v(d - 1, 0)
+                    gain_v(d - 1, 0)
+                elif gg == 1 and d < ND - 1:
                     for h in range(2):
                         add_v(d - 1, h)
                         gain_v(d - 1, h)
@@ -470,7 +471,6 @@ def tile_ternarylineartorch_kernel(tc, x, weight, bias, gamma, out):
                 if gg == 0:
                     passes_last(0, range(6))
                 else:
-                    passes_last(0, range(6, 8))
                     passes_last(1, range(8))
             else:
                 if gg == 0 and not transposed(d, 0):
@@ -483,11 +483,10 @@ def tile_ternarylineartorch_kernel(tc, x, weight, bias, gamma, out):
                 for h in range(2):
                     if gg == 1 and transposed(d, h):
                         s_first(d, h)
+            if gg == 0 and transposed(d - 1, 0):
                 for h in range(2):
-                    if gg == 0 and transposed(d - 1, h):
-                        back(d - 1, h)
+                    back(d - 1, h)
                 for h in range(2):
-                    if gg == 0 and transposed(d - 1, h):
-                        s_second(d - 1, h)
+                    s_second(d - 1, h)
         for h in range(2):
             last(h)

@@ -60,7 +60,7 @@ def tile_ternarylineartorch_kernel(tc, x, weight, bias, gamma, out):
         gam_f = const.tile([P, 1], F32, name="gam_f")
         brow_f = const.tile([P, P], F32, name="brow_f")
         bias_col = const.tile([P, 16], F32, name="bias_col")
-        ssum_sb = const.tile([P, NSUM], F32, name="ssum_sb")
+        ssum_sb = const.tile([P, 2], F32, name="ssum_sb")
         t_sb = const.tile([P, 1], F32, name="t_sb")
         t_low = const.tile([P, 1], I32, name="t_low")
         t_inv = const.tile([P, 1], F32, name="t_inv")
@@ -85,17 +85,17 @@ def tile_ternarylineartorch_kernel(tc, x, weight, bias, gamma, out):
             nc.scalar.copy(out=bias_bc[:, 512 * c : 512 * c + 512], in_=bb[:])
 
         w_t = [None] * NQ
-        w_sc = [keep.tile([P, 512], U8, name="w_sc%d" % q, align_bytes=64) for q in range(NQ)]
-        w_codes = [keep.tile([P, 512], U32, name="w_codes%d" % q, align_bytes=64) for q in range(NQ)]
-        x_codes = [keep.tile([P, 4, 512], U32, name="x_codes%d" % h, align_bytes=64) for h in range(2)]
-        x_sc = [keep.tile([P, 4, 512], U8, name="x_sc%d" % h, align_bytes=64) for h in range(2)]
+        w_sc = [keep.tile([P, 512], U8, name="w_sc%d" % q, align_bytes=256) for q in range(NQ)]
+        w_codes = [keep.tile([P, 512], U32, name="w_codes%d" % q, align_bytes=256) for q in range(NQ)]
+        x_codes = [keep.tile([P, 4, 512], U32, name="x_codes%d" % h, align_bytes=256) for h in range(2)]
+        x_sc = [keep.tile([P, 4, 512], U8, name="x_sc%d" % h, align_bytes=256) for h in range(2)]
 
         ssum_ps = bank(0, "ssum_ps")
 
         slot = [0]
 
         def stage(shape, name):
-            t = keep.tile(shape, BF16, name=name, tag="nat%d" % (slot[0] % 7), align_bytes=64)
+            t = keep.tile(shape, BF16, name=name, tag="nat%d" % (slot[0] % 6), align_bytes=64)
             slot[0] += 1
             return t
 
@@ -362,14 +362,17 @@ def tile_ternarylineartorch_kernel(tc, x, weight, bias, gamma, out):
                 )
 
         load_w_first(0)
-        for d in range(1, ND - 1):
+        for d in range(1, ND - 2):
             load_w(d)
         for d in range(ND - 1):
             if d == 0:
                 for gg in range(2):
                     w_abs("f%d" % gg, nats[gg][0].rearrange("p b k -> p (b k)").bitcast(I32))
-            else:
+            elif d < ND - 2:
                 w_abs(d, whole[d][:].rearrange("p b k -> p (b k)").bitcast(I32))
+            else:
+                for b in range(2):
+                    w_abs("g%d" % b, whole[d][:, b, :].bitcast(I32))
             if d == 2:
                 nc.vector.tensor_copy(out=bias_col[:], in_=bcs[0][:, 0:16])
             if d == 0:
@@ -379,26 +382,32 @@ def tile_ternarylineartorch_kernel(tc, x, weight, bias, gamma, out):
                 for key in range(4):
                     w_abs("h%d" % key, nats[NQ - 2 + key // 2][0][:, key % 2, :].bitcast(I32))
             for q in (2 * d, 2 * d + 1):
-                w_unit(q, [2 + (2 * q + gi) % 6 for gi in range(2)], (1,) if q % 2 == 1 and d < ND - 2 else ())
+                banks = [2 + (2 * q + gi) % 6 for gi in range(2)]
+                w_unit(q, banks, (1,) if q % 2 == 1 and d < ND - 2 else (), (0, 1) if q < NQ - 3 else (0,))
                 if d == 0:
                     w_sums("f%d" % q, first=(q == 0))
-            if d > 0:
+            if 0 < d < ND - 2:
                 w_sums(d)
+            elif d == ND - 2:
+                w_sums("g0")
+                w_sums("g1")
             if d == 0:
+                load_w(ND - 2)
+            if d == 1:
                 load_w_halves(ND - 1)
-            if 1 <= d <= 4:
-                load_x(d - 1)
+            if 2 <= d <= 5:
+                load_x(d - 2)
             if d == 1:
                 bc = bank(1, "bc")
                 nc.tensor.transpose(bc[:, 0:128], brow_f[:], ident[:])
                 bcs.append(bc)
         for key in range(4):
             w_sums("h%d" % key, end=(key == 3))
-        w_unit(NQ - 2, (2, 3), (), (0,))
-        nc.vector.tensor_copy(out=ssum_sb[:], in_=ssum_ps[:, 0:NSUM])
+        w_unit(NQ - 3, (4, 5), (), (1,))
+        nc.vector.tensor_copy(out=ssum_sb[:], in_=ssum_ps[:, 0:2])
         th2_ps = bank(1, "th2_ps")
-        nc.tensor.matmul(out=th2_ps[:, 0:NSUM], lhsT=ones_f[:], rhs=ssum_sb[:], start=True, stop=True)
-        w_unit(NQ - 2, (2, 3), (), (1,))
+        nc.tensor.matmul(out=th2_ps[:, 0:2], lhsT=ones_f[:], rhs=ssum_sb[:], start=True, stop=True)
+        w_unit(NQ - 2, (2, 3), ())
         w_unit(NQ - 1, (4, 5), ())
         nc.vector.tensor_scalar(
             out=t_sb[:], in0=th2_ps[:, 0:1], scalar1=0.5 / (N * K), scalar2=2.0**-100, op0=ALU.mult, op1=ALU.max

from contextlib import ExitStack

import concourse.mybir as mybir
from concourse.masks import make_identity

F32 = mybir.dt.float32
BF16 = mybir.dt.bfloat16
I32 = mybir.dt.int32
U32 = mybir.dt.uint32
U8 = mybir.dt.uint8
FP8X4 = mybir.dt.float8_e4m3fn_x4
ALU = mybir.AluOpType
ACT = mybir.ActivationFunctionType

P = 128
M, K, N = 1024, 2048, 2048
FLOPS = 2 * M * K * N
ABS_MASK = 0x7FFF7FFF
TOP_MASK = -0x3FFF4000
LOW16 = -65536
TWO = 2.0 / (1.0 + 2.0**-8)
NSUM = 48
ND = N // 256
NQ = 2 * ND
S_PAIRS = (0, 1, 3)
M_FIRST = 6
LEAD = 3
EARLY = 5


def tile_ternarylineartorch_kernel(tc, x, weight, bias, gamma, out):
    nc = tc.nc
    with ExitStack() as ctx:
        const = ctx.enter_context(tc.tile_pool(name="const", bufs=1))
        keep = ctx.enter_context(tc.tile_pool(name="keep", bufs=1))
        absp = ctx.enter_context(tc.tile_pool(name="absp", bufs=2))
        abs4 = ctx.enter_context(tc.tile_pool(name="abs4", bufs=4))
        xgp = ctx.enter_context(tc.tile_pool(name="xgp", bufs=1))
        yp = ctx.enter_context(tc.tile_pool(name="yp", bufs=2))
        psum = ctx.enter_context(tc.psum_pool(name="psum", bufs=1))
        ctx.enter_context(tc.manual_schedule())

        def bank(k, name):
            return psum.tile([P, 512], F32, tag="b%d" % k, name=name)

        ones_bf = const.tile([P, P], BF16, name="ones_bf")
        nc.vector.memset(ones_bf[:], 1.0)
        gam_bf = const.tile([P, 1], BF16, name="gam_bf")
        nc.sync.dma_start(out=gam_bf[:], in_=gamma.partition_broadcast(P))
        brow_bf = const.tile([P, P], BF16, name="brow_bf")
        nc.vector.memset(brow_bf[:], 0.0)
        nc.sync.dma_start(out=brow_bf[0:16, :], in_=bias.rearrange("(b p) -> b p", p=P))
        brow1 = keep.tile([P, N], BF16, name="brow1", tag="w_t15", align_bytes=64)
        nc.vector.memset(brow1[:], 0.0)
        nc.sync.dma_start(out=brow1[0:1, :], in_=bias.unsqueeze(0))
        ident = const.tile([P, P], F32, name="ident")
        make_identity(nc, ident[:])
        ones_f = const.tile([P, P], F32, name="ones_f")
        nc.vector.memset(ones_f[:], 1.0)
        gam_f = const.tile([P, 1], F32, name="gam_f")
        brow_f = const.tile([P, P], F32, name="brow_f")
        bias_col = const.tile([P, 16], F32, name="bias_col")
        ssum_sb = const.tile([P, 2], F32, name="ssum_sb")
        t_sb = const.tile([P, 1], F32, name="t_sb")
        t_low = const.tile([P, 1], I32, name="t_low")
        t_inv = const.tile([P, 1], F32, name="t_inv")
        s_sb = const.tile([P, 1], F32, name="s_sb")
        bias_bc = const.tile([P, N], BF16, name="bias_bc")

        ones_wide = keep.tile([P, 512], BF16, name="ones_wide", tag="w_t14", align_bytes=64)
        nc.vector.memset(ones_wide[:], 1.0)

        def keep_clock(n, k, rhs):
            for i in range(n):
                dummy = bank(k, "dummy")
                nc.tensor.matmul(out=dummy[:], lhsT=ones_bf[:], rhs=rhs[:, 0:512], start=True, stop=True)

        keep_clock(2, 1, ones_wide)

        for c in range(4):
            bb = bank((6, 7, 5, 4)[c], "bb")
            nc.tensor.matmul(
                out=bb[:], lhsT=ones_bf[:], rhs=brow1[:, 512 * c : 512 * c + 512], start=True, stop=True
            )
            nc.scalar.copy(out=bias_bc[:, 512 * c : 512 * c + 512], in_=bb[:])

        w_t = [None] * NQ
        w_sc = [keep.tile([P, 512], U8, name="w_sc%d" % q, align_bytes=256) for q in range(NQ)]
        w_codes = [keep.tile([P, 512], U32, name="w_codes%d" % q, align_bytes=256) for q in range(NQ)]
        x_codes = [keep.tile([P, 4, 512], U32, name="x_codes%d" % h, align_bytes=256) for h in range(2)]
        x_sc = [keep.tile([P, 4, 512], U8, name="x_sc%d" % h, align_bytes=256) for h in range(2)]

        ssum_ps = bank(0, "ssum_ps")

        slot = [0]

        def stage(shape, name):
            t = keep.tile(shape, BF16, name=name, tag="nat%d" % (slot[0] % 6), align_bytes=64)
            slot[0] += 1
            return t

        nats = {}
        whole = {}

        def load_w(d):
            nat = stage([P, 2, K], "wn")
            nc.sync.dma_start(out=nat[:], in_=weight[256 * d : 256 * d + 256, :].rearrange("(b p) k -> p b k", p=P))
            whole[d] = nat
            for gg in range(2):
                nats[2 * d + gg] = (nat, 512 * gg)

        def load_w_first(d):
            nat = stage([P, 2, 2, K // 2], "wf")
            for gg in range(2):
                src = weight[256 * d : 256 * d + 256, 1024 * gg : 1024 * gg + 1024]
                nc.sync.dma_start(out=nat[:, gg, :, :], in_=src.rearrange("(b p) k -> p b k", p=P))
                nats[2 * d + gg] = (nat[:, gg, :, :], 0)

        def load_w_halves(d):
            nat = stage([P, 2, 2, K // 2], "wh")
            for gg in range(2):
                for b in range(2):
                    r0 = 256 * d + 128 * b
                    nc.sync.dma_start(
                        out=nat[:, gg, b, :], in_=weight[r0 : r0 + 128, 1024 * gg : 1024 * gg + 1024]
                    )
                nats[2 * d + gg] = (nat[:, gg, :, :], 0)

        xnats = {}

        def load_x(ip):
            nat = stage([P, 2, 2, K // 2], "xn")
            for e in range(2):
                src = x[256 * ip : 256 * ip + 256, 1024 * e : 1024 * e + 1024]
                nc.sync.dma_start(out=nat[:, e, :, :], in_=src.rearrange("(b p) k -> p b k", p=P))
            xnats[ip] = nat

        def four_transposes(tp, sources):
            for j in range(4):
                nc.tensor.transpose(tp[:, 128 * j : 128 * j + 128], sources[j], ident[:])

        def copy_out(on_vector, tp, dst):
            src = tp[:].rearrange("p (b u r) -> p b r u", b=2, u=2)
            dst = dst.rearrange("p (b r u) -> p b r u", b=2, u=2)
            if on_vector:
                nc.vector.tensor_copy(out=dst, in_=src)
            else:
                nc.scalar.copy(out=dst, in_=src)

        def w_unit(q, banks, vector_banks, parts=(0, 1)):
            nat, base = nats[q]
            if 0 in parts:
                w_t[q] = keep.tile([P, 2048], BF16, name="w_t", tag="w_t%d" % q, align_bytes=64)
            for gi in parts:
                tp = bank(banks[gi], "wtp")
                srcs = []
                for b in range(2):
                    words = nat[:, b, :].bitcast(F32)
                    for u in range(2):
                        col = base + 256 * gi + 128 * u
                        srcs.append(words[:, col : col + 128])
                four_transposes(tp, srcs)
                copy_out(gi in vector_banks, tp, w_t[q][:].bitcast(F32)[:, 512 * gi : 512 * gi + 512])

        mags = {}
        bcs = []

        def w_abs(key, words):
            n = words.shape[-1]
            mag = (absp if n > 512 else abs4).tile([P, n], I32, name="mag", tag="mag" if n > 512 else "magq", align_bytes=64)
            nc.vector.tensor_scalar(out=mag[:], in0=words, scalar1=ABS_MASK, scalar2=None, op0=ALU.bitwise_and)
            mags[key] = mag

        def w_sums(key, first=False, end=False):
            cols = mags[key][:].bitcast(BF16)
            blocks = cols.shape[-1] // P
            for j in range(blocks):
                nc.tensor.matmul(
                    out=ssum_ps[:, 0:NSUM],
                    lhsT=cols[:, 128 * j : 128 * j + 128],
                    rhs=ones_bf[:, 0:NSUM],
                    start=(first and j == 0),
                    stop=(end and j == blocks - 1),
                )

        xg = xgp.tile([P, 4, 2, 512], F32, name="xg", align_bytes=64)

        def x_pair(ip, banks):
            for g in range(4):
                tp = bank(banks[g], "xtp")
                srcs = []
                for b in range(2):
                    words = xnats[ip][:, g // 2, b, :].bitcast(F32)
                    for u in range(2):
                        col = 256 * (g % 2) + 128 * u
                        srcs.append(words[:, col : col + 128])
                four_transposes(tp, srcs)
                copy_out(False, tp, xg[:, g, ip % 2, :])

        def x_quant(h):
            for g in range(4):
                nc.vector.quantize_mx(
                    out=x_codes[h][:, g, :].bitcast(FP8X4),
                    scales=x_sc[h][:, g, :],
                    in_=xg[:, g, :, :].rearrange("p t w -> p (t w)").bitcast(BF16),
                )

        def on_scalar(q):
            return q == EARLY or (q - LEAD >= M_FIRST and (q - LEAD) // 2 - 1 not in S_PAIRS)

        def scale_up(q):
            if on_scalar(q):
                nc.scalar.activation(out=w_t[q][:], in_=w_t[q][:], func=ACT.Copy, scale=s_sb[:, 0:1])
            else:
                nc.vector.tensor_scalar(
                    out=w_t[q][:], in0=w_t[q][:], scalar1=t_inv[:, 0:1], scalar2=TWO, op0=ALU.mult, op1=ALU.mult
                )

        def cut(q):
            words = w_t[q][:].bitcast(I32)
            nc.vector.tensor_scalar(out=words, in0=words, scalar1=TOP_MASK, scalar2=None, op0=ALU.bitwise_and)

        def halve(q):
            nc.vector.tensor_scalar(out=w_t[q][:], in0=w_t[q][:], scalar1=0.5, scalar2=None, op0=ALU.mult)

        def w_quant(q):
            nc.vector.quantize_mx(out=w_codes[q][:].bitcast(FP8X4), scales=w_sc[q][:], in_=w_t[q][:])

        def transposed(d, h):
            return d in S_PAIRS

        accs = {}

        def passes_s(q, h):
            d, gg = divmod(q, 2)
            for j in range(2):
                if gg == 0:
                    accs[(d, h, j)] = bank(4 * (d % 2) + 2 * h + j, "acc_s")
                for gi in range(2):
                    g = 2 * gg + gi
                    c0 = 256 * gi + 128 * j
                    nc.tensor.matmul_mx(
                        out=accs[(d, h, j)][:],
                        lhsT=w_codes[q][:, c0 : c0 + 128].bitcast(FP8X4),
                        lhsT_scale=w_sc[q][:, c0 : c0 + 128],
                        rhs=x_codes[h][:, g, :].bitcast(FP8X4),
                        rhs_scale=x_sc[h][:, g, :],
                        start=(g == 0),
                        stop=(g == 3),
                    )

        def pass_v(dst, d, h, j, g):
            q, gi = 2 * d + g // 2, g % 2
            nc.tensor.matmul_mx(
                out=dst,
                lhsT=x_codes[h][:, g, P * j : P * j + P].bitcast(FP8X4),
                lhsT_scale=x_sc[h][:, g, P * j : P * j + P],
                rhs=w_codes[q][:, 256 * gi : 256 * gi + 256].bitcast(FP8X4),
                rhs_scale=w_sc[q][:, 256 * gi : 256 * gi + 256],
                start=(g == 0),
                stop=(g == 3),
            )

        def passes_v_early(d):
            for h in range(2):
                for b in range(2):
                    acc = bank(4 * (d % 2) + 2 * h + b, "acc_v")
                    for g in range(2):
                        pass_v(acc[:, 0:256], d, h, 2 * b, g)
                    accs[(d, h, b)] = acc

        def passes_v(d, h):
            for b in range(2):
                acc = accs[(d, h, b)]
                for g in range(2, 4):
                    pass_v(acc[:, 0:256], d, h, 2 * b, g)
                for g in range(4):
                    pass_v(acc[:, 256:512], d, h, 2 * b + 1, g)

        def passes_last(gg, tiles):
            d = ND - 1
            for i in tiles:
                if gg == 0:
                    accs[(d, i)] = bank((4 + i) % 8, "acc_l")
                for gi in range(2):
                    pass_v(accs[(d, i)][:, 0:256], d, i // 4, i % 4, 2 * gg + gi)

        def rows(r0, nrows, d):
            return out[r0 : r0 + nrows, 256 * d : 256 * d + 256].rearrange("(t p) n -> p t n", p=P)

        def new_o(d, h):
            return keep.tile([P, 2, 512], F32, name="o", tag="w_t%d" % (2 * d + h), align_bytes=64)

        ovs = {}

        def add_v(d, h):
            o = new_o(d, h)
            bcast = bias_bc[:, 256 * d : 256 * d + 256].unsqueeze(1).to_broadcast([P, 2, 256])
            for b in range(2):
                nc.vector.tensor_tensor(
                    out=o[:, b, :].rearrange("p (t n) -> p t n", t=2),
                    in0=accs[(d, h, b)][:].rearrange("p (t n) -> p t n", t=2),
                    in1=bcast,
                    op=ALU.add,
                )
            ovs[(d, h)] = o

        def gain_v(d, h):
            o = ovs[(d, h)]
            for b in range(2):
                nc.scalar.activation(out=o[:, b, :], in_=o[:, b, :], func=ACT.Copy, scale=gam_f[:, 0:1])
                nc.sync.dma_start(
                    out=rows(512 * h + 256 * b, 256, d), in_=o[:, b, :].rearrange("p (t n) -> p t n", t=2)
                )

        def last(h):
            d = ND - 1
            o = new_o(d, h)
            for b in range(2):
                for t in range(2):
                    nc.vector.tensor_tensor(
                        out=o[:, b, 256 * t : 256 * t + 256],
                        in0=accs[(d, 4 * h + 2 * b + t)][:, 0:256],
                        in1=bias_bc[:, 256 * d : 256 * d + 256],
                        op=ALU.add,
                    )
                    piece = o[:, b, 256 * t : 256 * t + 256]
                    nc.scalar.activation(out=piece, in_=piece, func=ACT.Copy, scale=gam_f[:, 0:1])
                    r0 = 512 * h + 256 * b + 128 * t
                    nc.sync.dma_start(out=out[r0 : r0 + 128, 256 * d : 256 * d + 256], in_=piece)

        ys = {}

        def s_first(d, h):
            y = yp.tile([P, 2, 512], F32, name="y", align_bytes=64)
            for j in range(2):
                nb = 2 * d + j
                nc.scalar.activation(
                    out=y[:, j, :],
                    in_=accs[(d, h, j)][:],
                    func=ACT.Identity,
                    bias=bias_col[:, nb : nb + 1],
                    scale=1.0,
                )
            ys[(d, h)] = y

        backs = {}

        def back(d, h):
            for b in range(2):
                bt = bank(4 * (d % 2) + 2 * h + b, "bt")
                y = ys[(d, h)]
                four_transposes(bt, [y[:, j, 128 * (2 * b + t) : 128 * (2 * b + t) + 128] for t in range(2) for j in range(2)])
                backs[(d, h, b)] = bt

        def s_second(d, h):
            o = new_o(d, h)
            for b in range(2):
                nc.scalar.activation(out=o[:, b, :], in_=backs[(d, h, b)][:], func=ACT.Copy, scale=gam_f[:, 0:1])
                nc.sync.dma_start(
                    out=rows(512 * h + 256 * b, 256, d), in_=o[:, b, :].rearrange("p (t n) -> p t n", t=2)
                )

        load_w_first(0)
        for d in range(1, ND - 2):
            load_w(d)
        for d in range(ND - 1):
            if d == 0:
                for gg in range(2):
                    w_abs("f%d" % gg, nats[gg][0].rearrange("p b k -> p (b k)").bitcast(I32))
            elif d < ND - 2:
                w_abs(d, whole[d][:].rearrange("p b k -> p (b k)").bitcast(I32))
            else:
                for b in range(2):
                    w_abs("g%d" % b, whole[d][:, b, :].bitcast(I32))
            if d == 2:
                nc.vector.tensor_copy(out=bias_col[:], in_=bcs[0][:, 0:16])
            if d == 0:
                nc.vector.tensor_copy(out=gam_f[:], in_=gam_bf[:])
                nc.vector.tensor_copy(out=brow_f[:], in_=brow_bf[:])
            if d == ND - 2:
                for key in range(4):
                    w_abs("h%d" % key, nats[NQ - 2 + key // 2][0][:, key % 2, :].bitcast(I32))
            for q in (2 * d, 2 * d + 1):
                banks = [2 + (2 * q + gi) % 6 for gi in range(2)]
                w_unit(q, banks, (1,) if q % 2 == 1 and d < ND - 2 else (), (0, 1) if q < NQ - 3 else (0,))
                if d == 0:
                    w_sums("f%d" % q, first=(q == 0))
            if 0 < d < ND - 2:
                w_sums(d)
            elif d == ND - 2:
                w_sums("g0")
                w_sums("g1")
            if d == 0:
                load_w(ND - 2)
            if d == 1:
                load_w_halves(ND - 1)
            if 2 <= d <= 5:
                load_x(d - 2)
            if d == 1:
                bc = bank(1, "bc")
                nc.tensor.transpose(bc[:, 0:128], brow_f[:], ident[:])
                bcs.append(bc)
        for key in range(4):
            w_sums("h%d" % key, end=(key == 3))
        w_unit(NQ - 3, (4, 5), (), (1,))
        nc.vector.tensor_copy(out=ssum_sb[:], in_=ssum_ps[:, 0:2])
        th2_ps = bank(1, "th2_ps")
        nc.tensor.matmul(out=th2_ps[:, 0:2], lhsT=ones_f[:], rhs=ssum_sb[:], start=True, stop=True)
        w_unit(NQ - 2, (2, 3), ())
        w_unit(NQ - 1, (4, 5), ())
        nc.vector.tensor_scalar(
            out=t_sb[:], in0=th2_ps[:, 0:1], scalar1=0.5 / (N * K), scalar2=2.0**-100, op0=ALU.mult, op1=ALU.max
        )
        nc.vector.tensor_scalar(
            out=t_low[:], in0=t_sb[:].bitcast(I32), scalar1=LOW16, scalar2=None, op0=ALU.bitwise_and
        )
        nc.vector.reciprocal(out=t_inv[:], in_=t_low[:].bitcast(F32))
        x_pair(0, (6, 7, 2, 3))
        keep_clock(2, 0, bias_bc)
        x_pair(1, (4, 5, 6, 7))
        keep_clock(2, 0, bias_bc)

        scale_up(0)
        nc.vector.tensor_scalar(out=s_sb[:], in0=t_inv[:], scalar1=TWO, scalar2=None, op0=ALU.mult)
        cut(0)
        scale_up(1)
        halve(0)
        cut(1)
        w_quant(0)
        halve(1)
        scale_up(2)
        w_quant(1)
        x_quant(0)
        x_pair(2, (2, 3, 4, 5))
        keep_clock(1, 0, bias_bc)
        passes_s(0, 0)
        x_pair(3, (6, 7, 2, 3))
        passes_s(1, 0)
        s_first(0, 0)
        scale_up(EARLY)
        cut(2)
        scale_up(3)
        halve(2)
        cut(3)
        w_quant(2)
        passes_s(2, 0)
        x_quant(1)
        passes_s(0, 1)
        passes_s(1, 1)
        s_first(0, 1)
        passes_s(2, 1)
        back(0, 0)
        back(0, 1)
        s_second(0, 0)
        s_second(0, 1)
        for q in range(3, NQ):
            d, gg = divmod(q, 2)
            if q + 1 < NQ and not on_scalar(q + 1):
                scale_up(q + 1)
            halve(q)
            if q == NQ - 1:
                add_v(d - 1, 1)
                gain_v(d - 1, 1)
                passes_last(0, range(6, 8))
            if q + 1 < NQ:
                cut(q + 1)
            w_quant(q)
            if not transposed(d - 1, gg):
                if q + LEAD < NQ and on_scalar(q + LEAD):
                    scale_up(q + LEAD)
                if q == NQ - 2:
                    add_v(d - 1, 0)
                    gain_v(d - 1, 0)
                elif gg == 1 and d < ND - 1:
                    for h in range(2):
                        add_v(d - 1, h)
                        gain_v(d - 1, h)
            if d == ND - 1:
                if gg == 0:
                    passes_last(0, range(6))
                else:
                    passes_last(1, range(8))
            else:
                if gg == 0 and not transposed(d, 0):
                    passes_v_early(d)
                for h in range(2):
                    if transposed(d, h):
                        passes_s(q, h)
                    elif gg == 1:
                        passes_v(d, h)
                for h in range(2):
                    if gg == 1 and transposed(d, h):
                        s_first(d, h)
            if gg == 0 and transposed(d - 1, 0):
                for h in range(2):
                    back(d - 1, h)
                for h in range(2):
                    s_second(d - 1, h)
        for h in range(2):
            last(h)
